import numpy as np
import ml_dtypes


def mxq(x, axis, fmt="e4m3"):
    dtype, down = {"e4m3": (ml_dtypes.float8_e4m3fn, 7), "e5m2": (ml_dtypes.float8_e5m2, 14)}[fmt]
    v = np.moveaxis(np.asarray(x, np.float32).astype(ml_dtypes.bfloat16).astype(np.float64), axis, -1)
    blocks = v.reshape(v.shape[:-1] + (-1, 32))
    amax = np.abs(blocks).max(-1, keepdims=True)
    byte = np.maximum(np.where(amax > 0, np.frexp(amax)[1] - 1 + 127, 0) - down, 1)
    scale = np.exp2(byte - 127.0)
    codes = (blocks / scale).astype(np.float32).astype(dtype).astype(np.float64)
    return np.moveaxis((codes * scale).reshape(v.shape), -1, axis)


WIDE = False


def mx_kscale(k):
    if not WIDE:
        return np.ones(k)
    levels = np.array([10, -10, 5, -5, 0])
    if k % 512:
        return np.exp2(np.random.permutation(np.resize(levels, k // 32))).repeat(32)
    a = np.empty((k // 512, 16))
    for p in range(k // 512):
        a[p, :8] = np.random.permutation(np.resize(levels, 8))
        for g in range(8):
            far = levels[np.abs(levels - a[p, g]) >= 10]
            a[p, g + 8] = far[np.random.randint(len(far))]
    return np.exp2(a.ravel()).repeat(32)


BF16 = ml_dtypes.bfloat16


def bf(x):
    return np.asarray(x, np.float32).astype(BF16)


def f64(x):
    return np.asarray(x).astype(np.float64)


BW, NW, WZ, WH, WW, C, H, HD = 4, 2, 2, 8, 8, 1536, 32, 48
N = WZ * WH * WW
F = 3 * H * HD
SCALE = HD ** -0.5


def axis_rope(x, axis):
    d = x.shape[-1]
    L = x.shape[axis]
    inv_freq = 1.0 / (10000.0 ** (np.arange(0, d, 2) / d))
    ang = np.arange(L)[:, None] * inv_freq
    cos = np.concatenate([np.cos(ang), np.cos(ang)], -1)
    sin = np.concatenate([np.sin(ang), np.sin(ang)], -1)
    bshape = [1] * x.ndim
    bshape[axis] = L
    bshape[-1] = d
    cos = cos.reshape(bshape)
    sin = sin.reshape(bshape)
    x1, x2 = np.split(x, 2, axis=-1)
    rot = np.concatenate([-x2, x1], axis=-1)
    return x * cos + rot * sin


def rope3(x):
    d = x.shape[-1] // 3
    xz, xh, xw = x[..., :d], x[..., d:2 * d], x[..., 2 * d:]
    return np.concatenate([axis_rope(xz, 1), axis_rope(xh, 2), axis_rope(xw, 3)], -1)


def draw0():
    s = mx_kscale(C)
    return {"x": bf(np.random.standard_normal((BW, N, C)) * s),
            "qkv_w": bf(np.random.standard_normal((F, C)) / np.sqrt(C) / s),
            "qkv_b": bf(np.random.standard_normal(F) * 0.3)}


def core(x, qkv_w, qkv_b):
    y = (mxq(f64(x), 2, "e4m3") @ mxq(f64(qkv_w), 1, "e4m3").T) + f64(qkv_b)
    qkv = y.reshape(BW, N, 3, H, HD).transpose(2, 0, 3, 1, 4)
    q, k, v = qkv[0], qkv[1], qkv[2]
    q = rope3(q.reshape(-1, WZ, WH, WW, HD)).reshape(BW, H, N, HD)
    k = rope3(k.reshape(-1, WZ, WH, WW, HD)).reshape(BW, H, N, HD)
    return q * SCALE, k, np.ascontiguousarray(v)


def e4m3fn_bytes(y):
    return np.clip(np.asarray(y, np.float64), -448.0, 448.0).astype(np.float32).astype(ml_dtypes.float8_e4m3fn).view(np.uint8)


def e4m3fn_values(b):
    return np.asarray(b, np.uint8).view(ml_dtypes.float8_e4m3fn).astype(np.float64)


def setup_inputs():
    d = draw0()
    x0 = np.asarray(d['qkv_w']).astype(np.float64)
    s = (np.max(np.abs(x0), axis=(0,), keepdims=True) / 448.0).astype(np.float32)
    out = {}
    for k, v in d.items():
        if k == 'qkv_w':
            out['qkv_w_bytes'] = e4m3fn_bytes(x0 / s.astype(np.float64))
            out['qkv_w_scale'] = s
        else:
            out[k] = v
    return out


def reference(x, qkv_w_bytes, qkv_w_scale, qkv_b):
    return core(x, e4m3fn_values(qkv_w_bytes) * qkv_w_scale.astype(np.float64), qkv_b)

@@ -1,0 +1,427 @@
+import math
+from contextlib import ExitStack
+
+import concourse.mybir as mybir
+from concourse.masks import make_identity
+
+F32 = mybir.dt.float32
+BF16 = mybir.dt.bfloat16
+U32 = mybir.dt.uint32
+U8 = mybir.dt.uint8
+FP8 = mybir.dt.float8_e4m3fn
+FP8X4 = mybir.dt.float8_e4m3fn_x4
+ALU = mybir.AluOpType
+ACT = mybir.ActivationFunctionType
+AX = mybir.AxisListType
+
+P = 128
+K = 1536
+PASSES = 3
+NWIN = 4
+HEADS = 32
+HD = 48
+JROWS = HEADS * HD
+SCALE = HD ** -0.5
+OMEGA = [10000.0 ** (-i / 8.0) for i in range(8)]
+
+FLOPS = 2 * 512 * 4608 * 1536
+
+
+def pos_view(ap, third, pos):
+    if third == 0:
+        return ap.rearrange("p (a z y) -> p a z y", a=4, z=2)[:, :, pos, :]
+    if third == 1:
+        return ap.rearrange("p (az r y) -> p az r y", az=8, r=8)[:, :, pos, :]
+    return ap.rearrange("p (a zr wh win) -> p a zr wh win", a=4, zr=16, wh=2)[:, pos % 4, :, pos // 4, :]
+
+
+def tile_windowattention_pa_kernel(tc, x, qkv_w_bytes, qkv_w_scale, qkv_b, out_0, out_1, out_2):
+    nc = tc.nc
+    outs = [out_0, out_1, out_2]
+
+    with ExitStack() as ctx:
+        const = ctx.enter_context(tc.tile_pool(name="const", bufs=1))
+        xpool = ctx.enter_context(tc.tile_pool(name="xpool", bufs=1))
+        work = ctx.enter_context(tc.tile_pool(name="work", bufs=2))
+        ps_tp = ctx.enter_context(tc.psum_pool(name="ps_tp", bufs=4))
+        ps_mm = ctx.enter_context(tc.psum_pool(name="ps_mm", bufs=4))
+        ctx.enter_context(tc.manual_schedule())
+
+        w_j = [qkv_w_bytes[j * JROWS : (j + 1) * JROWS, :].rearrange("(p r) k -> p r k", r=12) for j in range(2)]
+        w_v = qkv_w_bytes[2 * JROWS :, :].rearrange("(c p) k -> p c k", p=P)
+
+        units = []
+        for j in range(2):
+            for rho in range(6):
+                units.append(("qk", j, rho))
+        for c in range(6):
+            units.append(("v", 2, c))
+        n_units = len(units)
+        st_bytes = {}
+
+        def load(i):
+            kind, j, idx = units[i]
+            src = w_j[j] if kind == "qk" else w_v
+            b_ = work.tile([P, 2, K], U8, name="wbytes", tag="wbytes", bufs=5)
+            nc.sync.dma_start(out=b_[:], in_=src[:, 2 * idx : 2 * idx + 2, :])
+            st_bytes[i] = b_
+
+        load(0)
+        sbc = const.tile([P, K], F32, name="sbc")
+        srow = qkv_w_scale.rearrange("o k -> (o k)")
+        for g in range(PASSES):
+            nc.sync.dma_start(out=sbc[:, 512 * g : 512 * (g + 1)], in_=srow[512 * g : 512 * (g + 1)].partition_broadcast(P))
+        load(1)
+        xb = []
+        for w in range(NWIN):
+            xt = xpool.tile([P, K], BF16, name="xb%d" % w)
+            nc.sync.dma_start(out=xt[:], in_=x[w])
+            xb.append(xt)
+        load(2)
+
+        rb = const.tile([P, P], BF16, name="rb")
+        nc.vector.memset(rb[:], 0.0)
+        for j in range(2):
+            nc.gpsimd.dma_start(
+                out=rb[12 * j : 12 * j + 12, :].rearrange("t (h e) -> t h e", e=4),
+                in_=qkv_b[j * JROWS : (j + 1) * JROWS].rearrange("(h t e) -> t h e", t=12, e=4),
+            )
+        bias_v = const.tile([P, HEADS, HD], BF16, name="bias_v")
+
+        ident_f = const.tile([P, P], F32, name="ident_f")
+        make_identity(nc, ident_f[:])
+        ident_b = const.tile([P, P], BF16, name="ident_b")
+        make_identity(nc, ident_b[:])
+
+        clsm = []
+        for c in range(1, 4):
+            m_ = const.tile([P, 1], F32, name="mask%d" % c)
+            nc.vector.tensor_reduce(
+                out=m_[:], in_=ident_f[:].rearrange("p (y four) -> p y four", four=4)[:, :, c], axis=AX.X, op=ALU.add
+            )
+            clsm.append(m_)
+        posrow = const.tile([P, 8], F32, name="posrow")
+        for pos in range(8):
+            nc.gpsimd.memset(posrow[:, pos : pos + 1], float(pos))
+        omega = []
+        for step in range(3):
+            om = const.tile([P, 2], F32, name="omega%d" % step)
+            omega.append(om)
+        angle = const.tile([P, 2, 2, 8], F32, name="angle")
+        wrap = const.tile([P, 2, 2, 8], F32, name="wrap")
+        trig = const.tile([P, 2, 2, 8], F32, name="trig")
+        cos_s = const.tile([P, 2, 2, 8], F32, name="cos_s")
+        sin_s = const.tile([P, 2, 2, 2, 8], F32, name="sin_s")
+
+        def trig_tables():
+            for step in range(3):
+                for iq in range(2):
+                    d_ = OMEGA[4 * iq + step + 1] - OMEGA[4 * iq]
+                    if step == 0:
+                        nc.scalar.activation(
+                            out=omega[0][:, iq : iq + 1], in_=clsm[0][:], func=ACT.Copy, scale=d_, bias=OMEGA[4 * iq]
+                        )
+                    else:
+                        nc.scalar.activation(
+                            out=omega[step][:, iq : iq + 1], in_=clsm[step][:], func=ACT.Identity, scale=d_,
+                            bias=omega[step - 1][:, iq : iq + 1],
+                        )
+            for iq in range(2):
+                nc.vector.tensor_scalar(
+                    out=angle[:, 0, iq, :], in0=posrow[:], scalar1=omega[2][:, iq : iq + 1], scalar2=math.pi / 2,
+                    op0=ALU.mult, op1=ALU.add,
+                )
+                nc.vector.tensor_scalar(
+                    out=angle[:, 1, iq, :], in0=posrow[:], scalar1=omega[2][:, iq : iq + 1], scalar2=None, op0=ALU.mult
+                )
+            nc.vector.tensor_scalar(
+                out=wrap[:], in0=angle[:], scalar1=math.pi, scalar2=-2.0 * math.pi, op0=ALU.is_gt, op1=ALU.mult
+            )
+            nc.vector.tensor_tensor(out=wrap[:], in0=wrap[:], in1=angle[:], op=ALU.add)
+            nc.scalar.activation(out=trig[:], in_=wrap[:], func=ACT.Sin)
+            for j in range(2):
+                sc = SCALE if j == 0 else 1.0
+                nc.scalar.activation(out=cos_s[:, j], in_=trig[:, 0], func=ACT.Copy, scale=sc)
+                nc.scalar.activation(out=sin_s[:, j, 0], in_=trig[:, 1], func=ACT.Copy, scale=-sc)
+                nc.scalar.activation(out=sin_s[:, j, 1], in_=trig[:, 1], func=ACT.Copy, scale=sc)
+
+        bt = const.tile([P, 24], F32, name="bt")
+        btab = const.tile([P, 24, 8], F32, name="btab")
+        tmpb = const.tile([P, 24, 8], F32, name="tmpb")
+
+        def bias_tables():
+            bps = ps_tp.tile([P, 512], F32, name="bps", tag="tp")
+            nc.tensor.matmul(out=bps[:, 0:24], lhsT=rb[:], rhs=ident_b[:, 0:24], start=True, stop=True)
+            nc.vector.tensor_copy(out=bt[:], in_=bps[:, 0:24])
+            for j in range(2):
+                btj = bt[:, 12 * j : 12 * j + 12]
+                nc.vector.tensor_tensor(
+                    out=btab[:, 12 * j : 12 * j + 12, :].rearrange("p (t6 iq) pos -> p t6 iq pos", iq=2),
+                    in0=cos_s[:, j].unsqueeze(1).to_broadcast([P, 6, 2, 8]),
+                    in1=btj.rearrange("p (t6 iq) -> p t6 iq", iq=2).unsqueeze(3).to_broadcast([P, 6, 2, 8]),
+                    op=ALU.mult,
+                )
+                for half in range(2):
+                    nc.vector.tensor_tensor(
+                        out=tmpb[:, 12 * j : 12 * j + 12, :].rearrange(
+                            "p (th hf iq) pos -> p th hf iq pos", hf=2, iq=2
+                        )[:, :, half],
+                        in0=sin_s[:, j, half].unsqueeze(1).to_broadcast([P, 3, 2, 8]),
+                        in1=btj.rearrange("p (th hf iq) -> p th hf iq", hf=2, iq=2)[:, :, 1 - half, :]
+                        .unsqueeze(3)
+                        .to_broadcast([P, 3, 2, 8]),
+                        op=ALU.mult,
+                    )
+            nc.vector.tensor_tensor(out=btab[:], in0=btab[:], in1=tmpb[:], op=ALU.add)
+
+        xcodes = const.tile([P, PASSES, 512], U32, name="xcodes", align_bytes=64)
+        xplanes = const.tile([P, PASSES, 512], U8, name="xplanes", align_bytes=64)
+
+        def x_pass(g):
+            gx = xpool.tile([P, 2048], BF16, name="gx", tag="gx", bufs=2, align_bytes=64)
+            gxw = gx[:].bitcast(F32).rearrange("p (a m wp y) -> p wp a m y", a=4, m=32, wp=2)
+            for wp in range(2):
+                wt = ps_tp.tile([P, 4, P], F32, name="wt", tag="tp")
+                for win2 in range(2):
+                    words = xb[2 * wp + win2][:].bitcast(F32)
+                    for u in range(2):
+                        nc.tensor.transpose(
+                            wt[:, 2 * win2 + u, :], words[:, 256 * g + u : 256 * (g + 1) : 2], ident_f[:]
+                        )
+                nc.scalar.copy(out=gxw[:, wp], in_=wt[:].rearrange("p y (m a) -> p a m y", a=4))
+            nc.vector.quantize_mx(out=xcodes[:, g, :].bitcast(FP8X4), scales=xplanes[:, g, :], in_=gx[:])
+
+        st_wb = {}
+        st_g = {}
+        st_codes = {}
+        o_qk = {}
+
+        def widen(i):
+            b_ = st_bytes[i]
+            wb = work.tile([P, 2, K], BF16, name="wb", tag="wb", bufs=3)
+            step = 512 if i == 0 else K
+            for c0 in range(0, K, step):
+                for r2 in range(2):
+                    nc.vector.tensor_tensor(
+                        out=wb[:, r2, c0 : c0 + step], in0=b_[:, r2, c0 : c0 + step].bitcast(FP8),
+                        in1=sbc[:, c0 : c0 + step], op=ALU.mult,
+                    )
+            st_wb[i] = wb
+
+        def turn(i):
+            kind, j, idx = units[i]
+            wb = st_wb[i]
+            if kind == "v" or idx % 2 == 0:
+                grp_new = work.tile([P, PASSES, 2048], BF16, name="grp", tag="grp", bufs=2, align_bytes=64)
+                st_g[(j, idx // 2 if kind == "qk" else idx)] = grp_new
+            grp = st_g[(j, idx // 2 if kind == "qk" else idx)]
+            for g in range(PASSES):
+                wt = ps_tp.tile([P, 4, P], F32, name="wt", tag="tp")
+                for r2 in range(2):
+                    words = wb[:, r2, :].bitcast(F32)
+                    for u in range(2):
+                        nc.tensor.transpose(
+                            wt[:, 2 * r2 + u, :], words[:, 256 * g + u : 256 * (g + 1) : 2], ident_f[:]
+                        )
+                if kind == "qk":
+                    gw = grp[:, g, :].bitcast(F32)
+                    nc.scalar.copy(
+                        out=gw.rearrange("p (cls h q2 y) -> p q2 cls h y", cls=4, h=HEADS, q2=2)[:, idx % 2],
+                        in_=wt[:].rearrange("p y (h cls) -> p cls h y", cls=4),
+                    )
+                else:
+                    gw = grp[:, g, 0:1024].bitcast(F32)
+                    nc.scalar.copy(
+                        out=gw.rearrange("p (c2 col u) -> p c2 col u", c2=2, u=2),
+                        in_=wt[:].rearrange("p (c2 u) col -> p c2 col u", u=2),
+                    )
+
+        def quant(j, idx, width):
+            grp = st_g[(j, idx)]
+            codes = work.tile([P, PASSES, 512], U32, name="codes", tag="codes", bufs=5, align_bytes=64)
+            planes = work.tile([P, PASSES, 512], U8, name="planes", tag="planes", bufs=5, align_bytes=64)
+            for g in range(PASSES):
+                nc.vector.quantize_mx(
+                    out=codes[:, g, 0 : width // 4].bitcast(FP8X4), scales=planes[:, g, 0 : width // 4],
+                    in_=grp[:, g, 0:width],
+                )
+            st_codes[(j, idx)] = (codes, planes)
+
+        def mx(j, idx, h):
+            codes, planes = st_codes[(j, idx)]
+            mm = ps_mm.tile([P, 512], F32, name="mm", tag="mm")
+            cols = slice(h * P, (h + 1) * P)
+            for g in range(PASSES):
+                nc.tensor.matmul_mx(
+                    out=mm[:],
+                    lhsT=codes[:, g, cols].bitcast(FP8X4), lhsT_scale=planes[:, g, cols],
+                    rhs=xcodes[:, g, :].bitcast(FP8X4), rhs_scale=xplanes[:, g, :],
+                    start=(g == 0), stop=(g == PASSES - 1),
+                )
+            return mm
+
+        def rope_s(j, t_lo):
+            third = t_lo // 4
+            iq = t_lo % 2
+            npos = 2 if third == 0 else 8
+            t_hi = t_lo + 2
+            mm_lo = mx(j, t_lo % 3, t_lo // 3)
+            mm_hi = mx(j, t_hi % 3, t_hi // 3)
+            jobs = []
+            for half, t, own, other in ((0, t_lo, mm_lo, mm_hi), (1, t_hi, mm_hi, mm_lo)):
+                o_ = work.tile([P, 512], F32, name="o", tag="o", bufs=14)
+                t_ = work.tile([P, 512], F32, name="t", tag="t", bufs=4)
+                nc.scalar.activation(
+                    out=pos_view(o_[:], third, 0), in_=pos_view(own[:], third, 0), func=ACT.Identity,
+                    scale=cos_s[:, j, iq, 0:1], bias=btab[:, 12 * j + t, 0:1],
+                )
+                for pos in range(1, npos):
+                    nc.scalar.activation(
+                        out=pos_view(t_[:], third, pos), in_=pos_view(other[:], third, pos), func=ACT.Identity,
+                        scale=sin_s[:, j, half, iq, pos : pos + 1], bias=btab[:, 12 * j + t, pos : pos + 1],
+                    )
+                o_qk[(j, t)] = o_
+                jobs.append((o_, t_, own))
+            return (j, third, iq, npos, jobs)
+
+        def rope_v(job):
+            j, third, iq, npos, jobs = job
+            for o_, t_, own in jobs:
+                for pos in range(1, npos):
+                    nc.vector.scalar_tensor_tensor(
+                        out=pos_view(o_[:], third, pos), in0=pos_view(own[:], third, pos),
+                        scalar=cos_s[:, j, iq, pos : pos + 1], in1=pos_view(t_[:], third, pos),
+                        op0=ALU.mult, op1=ALU.add,
+                    )
+
+        def copy_out(eng, out, in_):
+            if eng == "v":
+                nc.vector.tensor_copy(out=out, in_=in_)
+            else:
+                nc.scalar.copy(out=out, in_=in_)
+
+        stg_tiles = {}
+
+        def back_qk_bank(j, third, a, eng):
+            if third == 0 and a == 0:
+                stg_new = work.tile([P, HEADS, 4, HD], F32, name="stg", tag="stg", bufs=2)
+                stg_tiles[j] = stg_new
+            stg = stg_tiles[j]
+            tb = ps_tp.tile([P, 4, P], F32, name="tb", tag="tp")
+            for k4 in range(4):
+                nc.tensor.transpose(tb[:, k4, :], o_qk[(j, 4 * third + k4)][:, a * P : (a + 1) * P], ident_f[:])
+            copy_out(
+                eng,
+                stg[:, :, a, 16 * third : 16 * third + 16].rearrange("p h (k4 e4) -> p h k4 e4", e4=4),
+                tb[:].rearrange("p k4 (h e4) -> p h k4 e4", e4=4),
+            )
+            if third == 2 and a == 3:
+                for win in range(NWIN):
+                    nc.sync.dma_start(
+                        out=outs[j][win].rearrange("h (m a) e -> m h (a e)", a=4),
+                        in_=stg[win : P : 4, :, :, :].rearrange("p h a e -> p h (a e)"),
+                    )
+
+        def v_group(hg):
+            sv = work.tile([P, 8, 4, HD], F32, name="sv", tag="sv", bufs=2)
+            banks = []
+            for a in range(4):
+                mm = ps_mm.tile([P, 512], F32, name="mm", tag="mm")
+                toks = slice(a * P, (a + 1) * P)
+                for k3 in range(3):
+                    c = 3 * hg + k3
+                    codes, planes = st_codes[(2, c // 2)]
+                    cols = slice((c % 2) * P, (c % 2 + 1) * P)
+                    for g in range(PASSES):
+                        nc.tensor.matmul_mx(
+                            out=mm[:, k3 * P : (k3 + 1) * P],
+                            lhsT=xcodes[:, g, toks].bitcast(FP8X4), lhsT_scale=xplanes[:, g, toks],
+                            rhs=codes[:, g, cols].bitcast(FP8X4), rhs_scale=planes[:, g, cols],
+                            start=(g == 0), stop=(g == PASSES - 1),
+                        )
+                banks.append(mm)
+            return (hg, sv, banks)
+
+        def v_group_out(job):
+            hg, sv, banks = job
+            for a in range(4):
+                nc.vector.tensor_tensor(
+                    out=sv[:, :, a, :], in0=banks[a][:, 0 : 3 * P].rearrange("p (h e) -> p h e", e=HD),
+                    in1=bias_v[:, 8 * hg : 8 * hg + 8, :], op=ALU.add,
+                )
+            for win in range(NWIN):
+                nc.sync.dma_start(
+                    out=outs[2][win, 8 * hg : 8 * hg + 8].rearrange("h (m a) e -> m h (a e)", a=4),
+                    in_=sv[win : P : 4, :, :, :].rearrange("p h a e -> p h (a e)"),
+                )
+
+        mx_items = []
+        tb_items = []
+        mx_done = 0
+        tb_done = 0
+        pending_v = []
+        pending_g = []
+        widen(0)
+        for s in range(n_units + 4):
+            if s + 3 < n_units:
+                load(s + 3)
+            if s + 1 < n_units:
+                widen(s + 1)
+            for job in pending_v:
+                rope_v(job)
+            pending_v = []
+            for job in pending_g:
+                v_group_out(job)
+            pending_g = []
+            if s < n_units:
+                turn(s)
+            if s < PASSES:
+                x_pass(s)
+            if s == 1:
+                trig_tables()
+            if s == 2:
+                bias_tables()
+            if s == 4:
+                nc.sync.dma_start(
+                    out=bias_v[:].rearrange("p h e -> p (h e)"), in_=qkv_b[2 * JROWS :].partition_broadcast(P)
+                )
+            waiting = len(tb_items) - tb_done
+            n_tb = min(waiting, 4)
+            for k in range(n_tb):
+                item = tb_items[tb_done]
+                tb_done += 1
+                back_qk_bank(item[1], item[2], item[3], "s")
+            if s < n_units:
+                kind, j, idx = units[s]
+                if kind == "v":
+                    quant(2, idx, 1024)
+                elif idx % 2 == 1:
+                    quant(j, idx // 2, 2048)
+            banks_left = 4
+            while mx_done < len(mx_items) and banks_left >= (2 if mx_items[mx_done][0] == "pair" else 4):
+                item = mx_items[mx_done]
+                mx_done += 1
+                banks_left -= 2 if item[0] == "pair" else 4
+                if item[0] == "pair":
+                    j, t_lo = item[1], item[2]
+                    pending_v.append(rope_s(j, t_lo))
+                    if t_lo % 4 == item[3]:
+                        for a in range(4):
+                            tb_items.append(("qk", j, t_lo // 4, a))
+                else:
+                    pending_g.append(v_group(item[1]))
+            if s < n_units:
+                kind, j, idx = units[s]
+                if kind == "v":
+                    for hg in range(4):
+                        if (3 * hg + 2) // 2 == idx:
+                            mx_items.append(("v", hg))
+                elif idx == 3:
+                    mx_items.append(("pair", j, 1, 9))
+                    mx_items.append(("pair", j, 4, 9))
+                elif idx == 5:
+                    mx_items.append(("pair", j, 0, 0))
+                    mx_items.append(("pair", j, 5, 1))
+                    mx_items.append(("pair", j, 8, 9))
+                    mx_items.append(("pair", j, 9, 1))
+        assert mx_done == len(mx_items) and tb_done == len(tb_items) and len(pending_v) == 0 and len(pending_g) == 0

@@ -21,10 +21,14 @@ NWIN = 4
 HEADS = 32
 HD = 48
 JROWS = HEADS * HD
+HB = 16
+BROWS = HB * HD
 SCALE = HD ** -0.5
 OMEGA = [10000.0 ** (-i / 8.0) for i in range(8)]
 
 FLOPS = 2 * 512 * 4608 * 1536
+PE_SUM = (1, 2)
+TB_VECTOR = ((0, 0), (0, 1))
 
 
 def pos_view(ap, third, pos):
@@ -41,28 +45,27 @@ def tile_windowattention_pa_kernel(tc, x, qkv_w_bytes, qkv_w_scale, qkv_b, out_0
 
     with ExitStack() as ctx:
         const = ctx.enter_context(tc.tile_pool(name="const", bufs=1))
-        xpool = ctx.enter_context(tc.tile_pool(name="xpool", bufs=1))
         work = ctx.enter_context(tc.tile_pool(name="work", bufs=2))
         ps_tp = ctx.enter_context(tc.psum_pool(name="ps_tp", bufs=4))
         ps_mm = ctx.enter_context(tc.psum_pool(name="ps_mm", bufs=4))
         ctx.enter_context(tc.manual_schedule())
 
-        w_j = [qkv_w_bytes[j * JROWS : (j + 1) * JROWS, :].rearrange("(p r) k -> p r k", r=12) for j in range(2)]
+        w_blk = [qkv_w_bytes[b * BROWS : (b + 1) * BROWS, :].rearrange("(p r) k -> p r k", r=6) for b in range(4)]
         w_v = qkv_w_bytes[2 * JROWS :, :].rearrange("(c p) k -> p c k", p=P)
 
         units = []
-        for j in range(2):
-            for rho in range(6):
-                units.append(("qk", j, rho))
+        for blk in range(4):
+            for idx in range(3):
+                units.append(("qk", blk, idx))
         for c in range(6):
-            units.append(("v", 2, c))
+            units.append(("v", 4, c))
         n_units = len(units)
         st_bytes = {}
 
         def load(i):
-            kind, j, idx = units[i]
-            src = w_j[j] if kind == "qk" else w_v
-            b_ = work.tile([P, 2, K], U8, name="wbytes", tag="wbytes", bufs=5)
+            kind, blk, idx = units[i]
+            src = w_blk[blk] if kind == "qk" else w_v
+            b_ = work.tile([P, 2, K], U8, name="wbytes", tag="wbytes", bufs=4)
             nc.sync.dma_start(out=b_[:], in_=src[:, 2 * idx : 2 * idx + 2, :])
             st_bytes[i] = b_
 
@@ -72,19 +75,19 @@ def tile_windowattention_pa_kernel(tc, x, qkv_w_bytes, qkv_w_scale, qkv_b, out_0
         for g in range(PASSES):
             nc.sync.dma_start(out=sbc[:, 512 * g : 512 * (g + 1)], in_=srow[512 * g : 512 * (g + 1)].partition_broadcast(P))
         load(1)
-        xb = []
+        x_all = work.tile([P, NWIN, K], BF16, name="x_all", tag="stg", bufs=3, align_bytes=64)
+        gx_all = work.tile([P, 2, 2048], BF16, name="gx_all", tag="stg", bufs=3, align_bytes=64)
         for w in range(NWIN):
-            xt = xpool.tile([P, K], BF16, name="xb%d" % w)
-            nc.sync.dma_start(out=xt[:], in_=x[w])
-            xb.append(xt)
+            nc.sync.dma_start(out=x_all[:, w, :], in_=x[w])
         load(2)
 
+        rb0 = const.tile([P, P], BF16, name="rb0")
         rb = const.tile([P, P], BF16, name="rb")
-        nc.vector.memset(rb[:], 0.0)
-        for j in range(2):
+        nc.vector.memset(rb0[:], 0.0)
+        for blk in range(4):
             nc.gpsimd.dma_start(
-                out=rb[12 * j : 12 * j + 12, :].rearrange("t (h e) -> t h e", e=4),
-                in_=qkv_b[j * JROWS : (j + 1) * JROWS].rearrange("(h t e) -> t h e", t=12, e=4),
+                out=rb0[6 * blk : 6 * blk + 6, :].rearrange("t (h i) -> t h i", i=8),
+                in_=qkv_b[blk * BROWS : (blk + 1) * BROWS].rearrange("(h t i) -> t h i", t=6, i=8),
             )
         bias_v = const.tile([P, HEADS, HD], BF16, name="bias_v")
 
@@ -93,47 +96,29 @@ def tile_windowattention_pa_kernel(tc, x, qkv_w_bytes, qkv_w_scale, qkv_b, out_0
         ident_b = const.tile([P, P], BF16, name="ident_b")
         make_identity(nc, ident_b[:])
 
-        clsm = []
-        for c in range(1, 4):
-            m_ = const.tile([P, 1], F32, name="mask%d" % c)
-            nc.vector.tensor_reduce(
-                out=m_[:], in_=ident_f[:].rearrange("p (y four) -> p y four", four=4)[:, :, c], axis=AX.X, op=ALU.add
-            )
-            clsm.append(m_)
+        onehot = const.tile([P, 8], F32, name="onehot")
+        nc.vector.tensor_reduce(out=onehot[:], in_=ident_f[:].rearrange("p (c y) -> p c y", y=HB), axis=AX.X, op=ALU.add)
         posrow = const.tile([P, 8], F32, name="posrow")
         for pos in range(8):
             nc.gpsimd.memset(posrow[:, pos : pos + 1], float(pos))
-        omega = []
-        for step in range(3):
-            om = const.tile([P, 2], F32, name="omega%d" % step)
-            omega.append(om)
-        angle = const.tile([P, 2, 2, 8], F32, name="angle")
-        wrap = const.tile([P, 2, 2, 8], F32, name="wrap")
-        trig = const.tile([P, 2, 2, 8], F32, name="trig")
-        cos_s = const.tile([P, 2, 2, 8], F32, name="cos_s")
-        sin_s = const.tile([P, 2, 2, 2, 8], F32, name="sin_s")
+        omega = const.tile([P, 8], F32, name="omega")
+        angle = const.tile([P, 2, 8], F32, name="angle")
+        wrap = const.tile([P, 2, 8], F32, name="wrap")
+        trig = const.tile([P, 2, 8], F32, name="trig")
+        cos_s = const.tile([P, 2, 8], F32, name="cos_s")
+        sin_s = const.tile([P, 2, 2, 8], F32, name="sin_s")
 
         def trig_tables():
-            for step in range(3):
-                for iq in range(2):
-                    d_ = OMEGA[4 * iq + step + 1] - OMEGA[4 * iq]
-                    if step == 0:
-                        nc.scalar.activation(
-                            out=omega[0][:, iq : iq + 1], in_=clsm[0][:], func=ACT.Copy, scale=d_, bias=OMEGA[4 * iq]
-                        )
-                    else:
-                        nc.scalar.activation(
-                            out=omega[step][:, iq : iq + 1], in_=clsm[step][:], func=ACT.Identity, scale=d_,
-                            bias=omega[step - 1][:, iq : iq + 1],
-                        )
-            for iq in range(2):
-                nc.vector.tensor_scalar(
-                    out=angle[:, 0, iq, :], in0=posrow[:], scalar1=omega[2][:, iq : iq + 1], scalar2=math.pi / 2,
-                    op0=ALU.mult, op1=ALU.add,
+            nc.scalar.activation(out=omega[:, 0:1], in_=onehot[:, 0:1], func=ACT.Copy, scale=OMEGA[0])
+            for c in range(1, 8):
+                nc.scalar.activation(
+                    out=omega[:, c : c + 1], in_=onehot[:, c : c + 1], func=ACT.Identity, scale=OMEGA[c],
+                    bias=omega[:, c - 1 : c],
                 )
-                nc.vector.tensor_scalar(
-                    out=angle[:, 1, iq, :], in0=posrow[:], scalar1=omega[2][:, iq : iq + 1], scalar2=None, op0=ALU.mult
-                )
+            nc.vector.tensor_scalar(
+                out=angle[:, 0, :], in0=posrow[:], scalar1=omega[:, 7:8], scalar2=math.pi / 2, op0=ALU.mult, op1=ALU.add
+            )
+            nc.vector.tensor_scalar(out=angle[:, 1, :], in0=posrow[:], scalar1=omega[:, 7:8], scalar2=None, op0=ALU.mult)
             nc.vector.tensor_scalar(
                 out=wrap[:], in0=angle[:], scalar1=math.pi, scalar2=-2.0 * math.pi, op0=ALU.is_gt, op1=ALU.mult
             )
@@ -145,31 +130,35 @@ def tile_windowattention_pa_kernel(tc, x, qkv_w_bytes, qkv_w_scale, qkv_b, out_0
                 nc.scalar.activation(out=sin_s[:, j, 0], in_=trig[:, 1], func=ACT.Copy, scale=-sc)
                 nc.scalar.activation(out=sin_s[:, j, 1], in_=trig[:, 1], func=ACT.Copy, scale=sc)
 
+        tsin = {}
+        for third in PE_SUM:
+            for half in range(2):
+                ts_ = const.tile([P, 512], F32, name="tsin%d_%d" % (third, half))
+                nc.gpsimd.memset(pos_view(ts_[:], third, 0), 0.0)
+                tsin[(third, half)] = ts_
+
         bt = const.tile([P, 24], F32, name="bt")
         btab = const.tile([P, 24, 8], F32, name="btab")
         tmpb = const.tile([P, 24, 8], F32, name="tmpb")
 
         def bias_tables():
+            nc.vector.tensor_copy(out=rb[:].rearrange("p (i h) -> p i h", h=HB), in_=rb0[:].rearrange("p (h i) -> p i h", i=8))
             bps = ps_tp.tile([P, 512], F32, name="bps", tag="tp")
             nc.tensor.matmul(out=bps[:, 0:24], lhsT=rb[:], rhs=ident_b[:, 0:24], start=True, stop=True)
             nc.vector.tensor_copy(out=bt[:], in_=bps[:, 0:24])
             for j in range(2):
                 btj = bt[:, 12 * j : 12 * j + 12]
                 nc.vector.tensor_tensor(
-                    out=btab[:, 12 * j : 12 * j + 12, :].rearrange("p (t6 iq) pos -> p t6 iq pos", iq=2),
-                    in0=cos_s[:, j].unsqueeze(1).to_broadcast([P, 6, 2, 8]),
-                    in1=btj.rearrange("p (t6 iq) -> p t6 iq", iq=2).unsqueeze(3).to_broadcast([P, 6, 2, 8]),
+                    out=btab[:, 12 * j : 12 * j + 12, :],
+                    in0=cos_s[:, j].unsqueeze(1).to_broadcast([P, 12, 8]),
+                    in1=btj.unsqueeze(2).to_broadcast([P, 12, 8]),
                     op=ALU.mult,
                 )
                 for half in range(2):
                     nc.vector.tensor_tensor(
-                        out=tmpb[:, 12 * j : 12 * j + 12, :].rearrange(
-                            "p (th hf iq) pos -> p th hf iq pos", hf=2, iq=2
-                        )[:, :, half],
-                        in0=sin_s[:, j, half].unsqueeze(1).to_broadcast([P, 3, 2, 8]),
-                        in1=btj.rearrange("p (th hf iq) -> p th hf iq", hf=2, iq=2)[:, :, 1 - half, :]
-                        .unsqueeze(3)
-                        .to_broadcast([P, 3, 2, 8]),
+                        out=tmpb[:, 12 * j : 12 * j + 12, :].rearrange("p (q hf) pos -> p q hf pos", hf=2)[:, :, half],
+                        in0=sin_s[:, j, half].unsqueeze(1).to_broadcast([P, 6, 8]),
+                        in1=btj.rearrange("p (q hf) -> p q hf", hf=2)[:, :, 1 - half].unsqueeze(2).to_broadcast([P, 6, 8]),
                         op=ALU.mult,
                     )
             nc.vector.tensor_tensor(out=btab[:], in0=btab[:], in1=tmpb[:], op=ALU.add)
@@ -178,18 +167,18 @@ def tile_windowattention_pa_kernel(tc, x, qkv_w_bytes, qkv_w_scale, qkv_b, out_0
         xplanes = const.tile([P, PASSES, 512], U8, name="xplanes", align_bytes=64)
 
         def x_pass(g):
-            gx = xpool.tile([P, 2048], BF16, name="gx", tag="gx", bufs=2, align_bytes=64)
-            gxw = gx[:].bitcast(F32).rearrange("p (a m wp y) -> p wp a m y", a=4, m=32, wp=2)
+            gx = gx_all[:, g % 2, :]
+            gxw = gx.bitcast(F32).rearrange("p (a m wp y) -> p wp a m y", a=4, m=32, wp=2)
             for wp in range(2):
                 wt = ps_tp.tile([P, 4, P], F32, name="wt", tag="tp")
                 for win2 in range(2):
-                    words = xb[2 * wp + win2][:].bitcast(F32)
+                    words = x_all[:, 2 * wp + win2, :].bitcast(F32)
                     for u in range(2):
                         nc.tensor.transpose(
                             wt[:, 2 * win2 + u, :], words[:, 256 * g + u : 256 * (g + 1) : 2], ident_f[:]
                         )
                 nc.scalar.copy(out=gxw[:, wp], in_=wt[:].rearrange("p y (m a) -> p a m y", a=4))
-            nc.vector.quantize_mx(out=xcodes[:, g, :].bitcast(FP8X4), scales=xplanes[:, g, :], in_=gx[:])
+            nc.vector.quantize_mx(out=xcodes[:, g, :].bitcast(FP8X4), scales=xplanes[:, g, :], in_=gx)
 
         st_wb = {}
         st_g = {}
@@ -209,12 +198,12 @@ def tile_windowattention_pa_kernel(tc, x, qkv_w_bytes, qkv_w_scale, qkv_b, out_0
             st_wb[i] = wb
 
         def turn(i):
-            kind, j, idx = units[i]
+            kind, blk, idx = units[i]
             wb = st_wb[i]
-            if kind == "v" or idx % 2 == 0:
-                grp_new = work.tile([P, PASSES, 2048], BF16, name="grp", tag="grp", bufs=2, align_bytes=64)
-                st_g[(j, idx // 2 if kind == "qk" else idx)] = grp_new
-            grp = st_g[(j, idx // 2 if kind == "qk" else idx)]
+            if kind == "v" or idx == 0:
+                grp_new = work.tile([P, PASSES, 3072], BF16, name="grp", tag="grp", bufs=2, align_bytes=64)
+                st_g[(blk, idx if kind == "v" else 0)] = grp_new
+            grp = st_g[(blk, idx if kind == "v" else 0)]
             for g in range(PASSES):
                 wt = ps_tp.tile([P, 4, P], F32, name="wt", tag="tp")
                 for r2 in range(2):
@@ -224,11 +213,12 @@ def tile_windowattention_pa_kernel(tc, x, qkv_w_bytes, qkv_w_scale, qkv_b, out_0
                             wt[:, 2 * r2 + u, :], words[:, 256 * g + u : 256 * (g + 1) : 2], ident_f[:]
                         )
                 if kind == "qk":
-                    gw = grp[:, g, :].bitcast(F32)
-                    nc.scalar.copy(
-                        out=gw.rearrange("p (cls h q2 y) -> p q2 cls h y", cls=4, h=HEADS, q2=2)[:, idx % 2],
-                        in_=wt[:].rearrange("p y (h cls) -> p cls h y", cls=4),
-                    )
+                    gw = grp[:, g, :].bitcast(F32).rearrange("p (c8 r h u) -> p r c8 h u", c8=8, r=6, h=HB)
+                    for r2 in range(2):
+                        nc.scalar.copy(
+                            out=gw[:, 2 * idx + r2],
+                            in_=wt[:, 2 * r2 : 2 * r2 + 2, :].rearrange("p u (h c8) -> p c8 h u", c8=8),
+                        )
                 else:
                     gw = grp[:, g, 0:1024].bitcast(F32)
                     nc.scalar.copy(
@@ -236,21 +226,32 @@ def tile_windowattention_pa_kernel(tc, x, qkv_w_bytes, qkv_w_scale, qkv_b, out_0
                         in_=wt[:].rearrange("p (c2 u) col -> p c2 col u", u=2),
                     )
 
-        def quant(j, idx, width):
-            grp = st_g[(j, idx)]
-            codes = work.tile([P, PASSES, 512], U32, name="codes", tag="codes", bufs=5, align_bytes=64)
-            planes = work.tile([P, PASSES, 512], U8, name="planes", tag="planes", bufs=5, align_bytes=64)
+        def quant_qk(blk, third):
+            if third == 0:
+                codes_new = work.tile([P, PASSES, 768], U32, name="codes", tag="codes", bufs=2, align_bytes=64)
+                planes_new = work.tile([P, PASSES, 768], U8, name="planes", tag="planes", bufs=2, align_bytes=64)
+                st_codes[blk] = (codes_new, planes_new)
+            codes, planes = st_codes[blk]
+            grp = st_g[(blk, 0)]
+            cols = slice(256 * third, 256 * (third + 1))
             for g in range(PASSES):
                 nc.vector.quantize_mx(
-                    out=codes[:, g, 0 : width // 4].bitcast(FP8X4), scales=planes[:, g, 0 : width // 4],
-                    in_=grp[:, g, 0:width],
+                    out=codes[:, g, cols].bitcast(FP8X4), scales=planes[:, g, cols],
+                    in_=grp[:, g, 1024 * third : 1024 * (third + 1)],
                 )
-            st_codes[(j, idx)] = (codes, planes)
 
-        def mx(j, idx, h):
-            codes, planes = st_codes[(j, idx)]
+        def quant_v(c):
+            grp = st_g[(4, c)]
+            codes = work.tile([P, PASSES, 256], U32, name="vcodes", tag="vcodes", bufs=4, align_bytes=64)
+            planes = work.tile([P, PASSES, 256], U8, name="vplanes", tag="vplanes", bufs=4, align_bytes=64)
+            for g in range(PASSES):
+                nc.vector.quantize_mx(out=codes[:, g, :].bitcast(FP8X4), scales=planes[:, g, :], in_=grp[:, g, 0:1024])
+            st_codes[(4, c)] = (codes, planes)
+
+        def mx(blk, tile_no):
+            codes, planes = st_codes[blk]
             mm = ps_mm.tile([P, 512], F32, name="mm", tag="mm")
-            cols = slice(h * P, (h + 1) * P)
+            cols = slice(tile_no * P, (tile_no + 1) * P)
             for g in range(PASSES):
                 nc.tensor.matmul_mx(
                     out=mm[:],
@@ -260,109 +261,139 @@ def tile_windowattention_pa_kernel(tc, x, qkv_w_bytes, qkv_w_scale, qkv_b, out_0
                 )
             return mm
 
-        def rope_s(j, t_lo):
-            third = t_lo // 4
-            iq = t_lo % 2
+        def pair_mx(blk, third):
+            return (blk, third, mx(blk, 2 * third), mx(blk, 2 * third + 1))
+
+        def rope_s(pair):
+            blk, third, mm_lo, mm_hi = pair
+            j = blk // 2
             npos = 2 if third == 0 else 8
-            t_hi = t_lo + 2
-            mm_lo = mx(j, t_lo % 3, t_lo // 3)
-            mm_hi = mx(j, t_hi % 3, t_hi // 3)
             jobs = []
-            for half, t, own, other in ((0, t_lo, mm_lo, mm_hi), (1, t_hi, mm_hi, mm_lo)):
-                o_ = work.tile([P, 512], F32, name="o", tag="o", bufs=14)
-                t_ = work.tile([P, 512], F32, name="t", tag="t", bufs=4)
+            for half, own, other in ((0, mm_lo, mm_hi), (1, mm_hi, mm_lo)):
+                col = 6 * blk + 2 * third + half
+                o_ = work.tile([P, 512], F32, name="o", tag="o", bufs=4)
+                o_qk[(blk, third, half)] = o_
+                if third in PE_SUM:
+                    for pos in range(npos):
+                        nc.scalar.activation(
+                            out=pos_view(o_[:], third, pos), in_=pos_view(own[:], third, pos), func=ACT.Identity,
+                            scale=cos_s[:, j, pos : pos + 1], bias=btab[:, col, pos : pos + 1],
+                        )
+                    for pos in range(1, npos):
+                        nc.scalar.activation(
+                            out=pos_view(tsin[(third, half)][:], third, pos), in_=pos_view(other[:], third, pos),
+                            func=ACT.Copy, scale=sin_s[:, j, half, pos : pos + 1],
+                        )
+                    continue
+                t_ = work.tile([P, 512], F32, name="t", tag="t", bufs=2)
                 nc.scalar.activation(
                     out=pos_view(o_[:], third, 0), in_=pos_view(own[:], third, 0), func=ACT.Identity,
-                    scale=cos_s[:, j, iq, 0:1], bias=btab[:, 12 * j + t, 0:1],
+                    scale=cos_s[:, j, 0:1], bias=btab[:, col, 0:1],
                 )
                 for pos in range(1, npos):
                     nc.scalar.activation(
                         out=pos_view(t_[:], third, pos), in_=pos_view(other[:], third, pos), func=ACT.Identity,
-                        scale=sin_s[:, j, half, iq, pos : pos + 1], bias=btab[:, 12 * j + t, pos : pos + 1],
+                        scale=sin_s[:, j, half, pos : pos + 1], bias=btab[:, col, pos : pos + 1],
                     )
-                o_qk[(j, t)] = o_
                 jobs.append((o_, t_, own))
-            return (j, third, iq, npos, jobs)
+            return (j, third, npos, jobs)
 
         def rope_v(job):
-            j, third, iq, npos, jobs = job
+            j, third, npos, jobs = job
             for o_, t_, own in jobs:
                 for pos in range(1, npos):
                     nc.vector.scalar_tensor_tensor(
                         out=pos_view(o_[:], third, pos), in0=pos_view(own[:], third, pos),
-                        scalar=cos_s[:, j, iq, pos : pos + 1], in1=pos_view(t_[:], third, pos),
+                        scalar=cos_s[:, j, pos : pos + 1], in1=pos_view(t_[:], third, pos),
                         op0=ALU.mult, op1=ALU.add,
                     )
 
-        def copy_out(eng, out, in_):
-            if eng == "v":
-                nc.vector.tensor_copy(out=out, in_=in_)
-            else:
-                nc.scalar.copy(out=out, in_=in_)
-
         stg_tiles = {}
 
-        def back_qk_bank(j, third, a, eng):
-            if third == 0 and a == 0:
-                stg_new = work.tile([P, HEADS, 4, HD], F32, name="stg", tag="stg", bufs=2)
-                stg_tiles[j] = stg_new
-            stg = stg_tiles[j]
-            tb = ps_tp.tile([P, 4, P], F32, name="tb", tag="tp")
-            for k4 in range(4):
-                nc.tensor.transpose(tb[:, k4, :], o_qk[(j, 4 * third + k4)][:, a * P : (a + 1) * P], ident_f[:])
-            copy_out(
-                eng,
-                stg[:, :, a, 16 * third : 16 * third + 16].rearrange("p h (k4 e4) -> p h k4 e4", e4=4),
-                tb[:].rearrange("p k4 (h e4) -> p h k4 e4", e4=4),
-            )
-            if third == 2 and a == 3:
+        def back_t(blk, third, ah):
+            tb = ps_tp.tile([P, 2, 2, P], F32, name="tb", tag="tp")
+            for a2 in range(2):
+                toks = slice((2 * ah + a2) * P, (2 * ah + a2 + 1) * P)
+                for half in range(2):
+                    if third in PE_SUM:
+                        nc.tensor.matmul(
+                            out=tb[:, a2, half, :], lhsT=o_qk[(blk, third, half)][:, toks], rhs=ident_f[:],
+                            is_transpose=True, start=True, stop=False,
+                        )
+                        nc.tensor.matmul(
+                            out=tb[:, a2, half, :], lhsT=tsin[(third, half)][:, toks], rhs=ident_f[:],
+                            is_transpose=True, start=False, stop=True,
+                        )
+                    else:
+                        nc.tensor.transpose(tb[:, a2, half, :], o_qk[(blk, third, half)][:, toks], ident_f[:])
+            return (blk, third, ah, tb)
+
+        def back_out(job):
+            blk, third, ah, tb = job
+            if third == 0 and ah == 0:
+                stg_new = work.tile([P, HB, 4, HD], F32, name="stg", tag="stg", bufs=3, align_bytes=64)
+                stg_tiles[blk] = stg_new
+            stg = stg_tiles[blk]
+            dst = stg[:, :, 2 * ah : 2 * ah + 2, 16 * third : 16 * third + 16]
+            src = tb[:].rearrange("p a2 hf (i h) -> p h a2 (hf i)", h=HB)
+            if (third, ah) in TB_VECTOR:
+                nc.vector.tensor_copy(out=dst, in_=src)
+            else:
+                nc.scalar.copy(out=dst, in_=src)
+            if third == 2 and ah == 1:
+                j, hh = blk // 2, blk % 2
                 for win in range(NWIN):
                     nc.sync.dma_start(
-                        out=outs[j][win].rearrange("h (m a) e -> m h (a e)", a=4),
+                        out=outs[j][win, HB * hh : HB * (hh + 1)].rearrange("h (m a) e -> m h (a e)", a=4),
                         in_=stg[win : P : 4, :, :, :].rearrange("p h a e -> p h (a e)"),
                     )
 
-        def v_group(hg):
-            sv = work.tile([P, 8, 4, HD], F32, name="sv", tag="sv", bufs=2)
-            banks = []
-            for a in range(4):
-                mm = ps_mm.tile([P, 512], F32, name="mm", tag="mm")
-                toks = slice(a * P, (a + 1) * P)
-                for k3 in range(3):
-                    c = 3 * hg + k3
-                    codes, planes = st_codes[(2, c // 2)]
-                    cols = slice((c % 2) * P, (c % 2 + 1) * P)
-                    for g in range(PASSES):
-                        nc.tensor.matmul_mx(
-                            out=mm[:, k3 * P : (k3 + 1) * P],
-                            lhsT=xcodes[:, g, toks].bitcast(FP8X4), lhsT_scale=xplanes[:, g, toks],
-                            rhs=codes[:, g, cols].bitcast(FP8X4), rhs_scale=planes[:, g, cols],
-                            start=(g == 0), stop=(g == PASSES - 1),
-                        )
-                banks.append(mm)
-            return (hg, sv, banks)
+        sv_tiles = {}
 
-        def v_group_out(job):
-            hg, sv, banks = job
-            for a in range(4):
-                nc.vector.tensor_tensor(
-                    out=sv[:, :, a, :], in0=banks[a][:, 0 : 3 * P].rearrange("p (h e) -> p h e", e=HD),
-                    in1=bias_v[:, 8 * hg : 8 * hg + 8, :], op=ALU.add,
-                )
-            for win in range(NWIN):
-                nc.sync.dma_start(
-                    out=outs[2][win, 8 * hg : 8 * hg + 8].rearrange("h (m a) e -> m h (a e)", a=4),
-                    in_=sv[win : P : 4, :, :, :].rearrange("p h a e -> p h (a e)"),
-                )
+        def v_bank(hg, a):
+            if a == 0:
+                sv_new = work.tile([P, 8, 4, HD], F32, name="sv", tag="sv", bufs=4)
+                sv_tiles[hg] = sv_new
+            mm = ps_mm.tile([P, 512], F32, name="mm", tag="mm")
+            toks = slice(a * P, (a + 1) * P)
+            for k3 in range(3):
+                c = 3 * hg + k3
+                codes, planes = st_codes[(4, c // 2)]
+                cols = slice((c % 2) * P, (c % 2 + 1) * P)
+                for g in range(PASSES):
+                    nc.tensor.matmul_mx(
+                        out=mm[:, k3 * P : (k3 + 1) * P],
+                        lhsT=xcodes[:, g, toks].bitcast(FP8X4), lhsT_scale=xplanes[:, g, toks],
+                        rhs=codes[:, g, cols].bitcast(FP8X4), rhs_scale=planes[:, g, cols],
+                        start=(g == 0), stop=(g == PASSES - 1),
+                    )
+            return (hg, a, mm)
 
-        mx_items = []
-        tb_items = []
-        mx_done = 0
-        tb_done = 0
+        def v_bank_out(job):
+            hg, a, mm = job
+            sv = sv_tiles[hg]
+            nc.vector.tensor_tensor(
+                out=sv[:, :, a, :], in0=mm[:, 0 : 3 * P].rearrange("p (h e) -> p h e", e=HD),
+                in1=bias_v[:, 8 * hg : 8 * hg + 8, :], op=ALU.add,
+            )
+            if a == 3:
+                for win in range(NWIN):
+                    nc.sync.dma_start(
+                        out=outs[2][win, 8 * hg : 8 * hg + 8].rearrange("h (m a) e -> m h (a e)", a=4),
+                        in_=sv[win : P : 4, :, :, :].rearrange("p h a e -> p h (a e)"),
+                    )
+
+        quant_items = []
+        pair_items = []
+        v_items = []
+        quant_done = 0
+        pair_done = 0
+        v_done = 0
+        back_pair = None
         pending_v = []
         pending_g = []
         widen(0)
-        for s in range(n_units + 4):
+        for s in range(n_units + 3):
             if s + 3 < n_units:
                 load(s + 3)
             if s + 1 < n_units:
@@ -371,7 +402,7 @@ def tile_windowattention_pa_kernel(tc, x, qkv_w_bytes, qkv_w_scale, qkv_b, out_0
                 rope_v(job)
             pending_v = []
             for job in pending_g:
-                v_group_out(job)
+                v_bank_out(job)
             pending_g = []
             if s < n_units:
                 turn(s)
@@ -385,43 +416,45 @@ def tile_windowattention_pa_kernel(tc, x, qkv_w_bytes, qkv_w_scale, qkv_b, out_0
                 nc.sync.dma_start(
                     out=bias_v[:].rearrange("p h e -> p (h e)"), in_=qkv_b[2 * JROWS :].partition_broadcast(P)
                 )
-            waiting = len(tb_items) - tb_done
-            n_tb = min(waiting, 4)
-            for k in range(n_tb):
-                item = tb_items[tb_done]
-                tb_done += 1
-                back_qk_bank(item[1], item[2], item[3], "s")
-            if s < n_units:
-                kind, j, idx = units[s]
-                if kind == "v":
-                    quant(2, idx, 1024)
-                elif idx % 2 == 1:
-                    quant(j, idx // 2, 2048)
             banks_left = 4
-            while mx_done < len(mx_items) and banks_left >= (2 if mx_items[mx_done][0] == "pair" else 4):
-                item = mx_items[mx_done]
-                mx_done += 1
-                banks_left -= 2 if item[0] == "pair" else 4
-                if item[0] == "pair":
-                    j, t_lo = item[1], item[2]
-                    pending_v.append(rope_s(j, t_lo))
-                    if t_lo % 4 == item[3]:
-                        for a in range(4):
-                            tb_items.append(("qk", j, t_lo // 4, a))
-                else:
-                    pending_g.append(v_group(item[1]))
+            pair = None
+            if pair_done < len(pair_items):
+                pair = pair_mx(pair_items[pair_done][0], pair_items[pair_done][1])
+                pair_done += 1
+                banks_left -= 2
+            while banks_left > 0 and v_done < len(v_items):
+                pending_g.append(v_bank(v_items[v_done][0], v_items[v_done][1]))
+                v_done += 1
+                banks_left -= 1
+            back_jobs = []
+            if back_pair is not None:
+                back_jobs = [back_t(back_pair[0], back_pair[1], ah) for ah in range(2)]
+            back_pair = None
+            for job in back_jobs:
+                if (job[1], job[2]) in TB_VECTOR:
+                    back_out(job)
             if s < n_units:
-                kind, j, idx = units[s]
+                kind, blk, idx = units[s]
                 if kind == "v":
+                    quant_v(idx)
                     for hg in range(4):
                         if (3 * hg + 2) // 2 == idx:
-                            mx_items.append(("v", hg))
-                elif idx == 3:
-                    mx_items.append(("pair", j, 1, 9))
-                    mx_items.append(("pair", j, 4, 9))
-                elif idx == 5:
-                    mx_items.append(("pair", j, 0, 0))
-                    mx_items.append(("pair", j, 5, 1))
-                    mx_items.append(("pair", j, 8, 9))
-                    mx_items.append(("pair", j, 9, 1))
-        assert mx_done == len(mx_items) and tb_done == len(tb_items) and len(pending_v) == 0 and len(pending_g) == 0
+                            for a in range(4):
+                                v_items.append((hg, a))
+                elif idx == 2:
+                    for third in range(3):
+                        quant_items.append((blk, third))
+            if quant_done < len(quant_items):
+                quant_qk(quant_items[quant_done][0], quant_items[quant_done][1])
+                pair_items.append(quant_items[quant_done])
+                quant_done += 1
+            if pair is not None:
+                job = rope_s(pair)
+                if pair[1] not in PE_SUM:
+                    pending_v.append(job)
+                back_pair = (pair[0], pair[1])
+            for job in back_jobs:
+                if (job[1], job[2]) not in TB_VECTOR:
+                    back_out(job)
+        assert quant_done == len(quant_items) and pair_done == len(pair_items) and v_done == len(v_items)
+        assert len(pending_v) == 0 and len(pending_g) == 0 and back_pair is None

@@ -29,6 +29,7 @@ OMEGA = [10000.0 ** (-i / 8.0) for i in range(8)]
 FLOPS = 2 * 512 * 4608 * 1536
 PE_SUM = (1, 2)
 TB_VECTOR = ((0, 0), (0, 1))
+V_BANKS_SLOT = 4
 
 
 def pos_view(ap, third, pos):
@@ -69,6 +70,11 @@ def tile_windowattention_pa_kernel(tc, x, qkv_w_bytes, qkv_w_scale, qkv_b, out_0
             nc.sync.dma_start(out=b_[:], in_=src[:, 2 * idx : 2 * idx + 2, :])
             st_bytes[i] = b_
 
+        ident_f = const.tile([P, P], F32, name="ident_f")
+        make_identity(nc, ident_f[:])
+        ident_b = const.tile([P, P], BF16, name="ident_b")
+        make_identity(nc, ident_b[:])
+
         load(0)
         sbc = const.tile([P, K], F32, name="sbc")
         srow = qkv_w_scale.rearrange("o k -> (o k)")
@@ -90,11 +96,6 @@ def tile_windowattention_pa_kernel(tc, x, qkv_w_bytes, qkv_w_scale, qkv_b, out_0
                 in_=qkv_b[blk * BROWS : (blk + 1) * BROWS].rearrange("(h t i) -> t h i", t=6, i=8),
             )
         bias_v = const.tile([P, HEADS, HD], BF16, name="bias_v")
-
-        ident_f = const.tile([P, P], F32, name="ident_f")
-        make_identity(nc, ident_f[:])
-        ident_b = const.tile([P, P], BF16, name="ident_b")
-        make_identity(nc, ident_b[:])
 
         onehot = const.tile([P, 8], F32, name="onehot")
         nc.vector.tensor_reduce(out=onehot[:], in_=ident_f[:].rearrange("p (c y) -> p c y", y=HB), axis=AX.X, op=ALU.add)
@@ -178,7 +179,9 @@ def tile_windowattention_pa_kernel(tc, x, qkv_w_bytes, qkv_w_scale, qkv_b, out_0
                             wt[:, 2 * win2 + u, :], words[:, 256 * g + u : 256 * (g + 1) : 2], ident_f[:]
                         )
                 nc.scalar.copy(out=gxw[:, wp], in_=wt[:].rearrange("p y (m a) -> p a m y", a=4))
-            nc.vector.quantize_mx(out=xcodes[:, g, :].bitcast(FP8X4), scales=xplanes[:, g, :], in_=gx)
+
+        def x_quant(g):
+            nc.vector.quantize_mx(out=xcodes[:, g, :].bitcast(FP8X4), scales=xplanes[:, g, :], in_=gx_all[:, g % 2, :])
 
         st_wb = {}
         st_g = {}
@@ -390,24 +393,24 @@ def tile_windowattention_pa_kernel(tc, x, qkv_w_bytes, qkv_w_scale, qkv_b, out_0
         pair_done = 0
         v_done = 0
         back_pair = None
+        fresh_v = []
+        fresh_pairs = []
         pending_v = []
-        pending_g = []
         widen(0)
         for s in range(n_units + 3):
             if s + 3 < n_units:
                 load(s + 3)
+            if s < n_units:
+                turn(s)
+            if s < PASSES:
+                x_pass(s)
             if s + 1 < n_units:
                 widen(s + 1)
             for job in pending_v:
                 rope_v(job)
             pending_v = []
-            for job in pending_g:
-                v_bank_out(job)
-            pending_g = []
-            if s < n_units:
-                turn(s)
             if s < PASSES:
-                x_pass(s)
+                x_quant(s)
             if s == 1:
                 trig_tables()
             if s == 2:
@@ -416,14 +419,39 @@ def tile_windowattention_pa_kernel(tc, x, qkv_w_bytes, qkv_w_scale, qkv_b, out_0
                 nc.sync.dma_start(
                     out=bias_v[:].rearrange("p h e -> p (h e)"), in_=qkv_b[2 * JROWS :].partition_broadcast(P)
                 )
-            banks_left = 4
+            for item in fresh_v:
+                v_items.append(item)
+            fresh_v = []
+            for item in fresh_pairs:
+                pair_items.append(item)
+            fresh_pairs = []
+            if s < n_units:
+                kind, blk, idx = units[s]
+                if kind == "v":
+                    quant_v(idx)
+                    for hg in range(4):
+                        if (3 * hg + 2) // 2 == idx:
+                            for a in range(4):
+                                fresh_v.append((hg, a))
+                elif idx == 2:
+                    for third in range(3):
+                        quant_items.append((blk, third))
+            if quant_done < len(quant_items):
+                quant_qk(quant_items[quant_done][0], quant_items[quant_done][1])
+                fresh_pairs.append(quant_items[quant_done])
+                quant_done += 1
+            if s == n_units - 1:
+                for item in fresh_v:
+                    v_items.append(item)
+                fresh_v = []
+            banks_left = V_BANKS_SLOT if s < n_units - 1 else 8
             pair = None
             if pair_done < len(pair_items):
                 pair = pair_mx(pair_items[pair_done][0], pair_items[pair_done][1])
                 pair_done += 1
                 banks_left -= 2
             while banks_left > 0 and v_done < len(v_items):
-                pending_g.append(v_bank(v_items[v_done][0], v_items[v_done][1]))
+                v_bank_out(v_bank(v_items[v_done][0], v_items[v_done][1]))
                 v_done += 1
                 banks_left -= 1
             back_jobs = []
@@ -433,21 +461,6 @@ def tile_windowattention_pa_kernel(tc, x, qkv_w_bytes, qkv_w_scale, qkv_b, out_0
             for job in back_jobs:
                 if (job[1], job[2]) in TB_VECTOR:
                     back_out(job)
-            if s < n_units:
-                kind, blk, idx = units[s]
-                if kind == "v":
-                    quant_v(idx)
-                    for hg in range(4):
-                        if (3 * hg + 2) // 2 == idx:
-                            for a in range(4):
-                                v_items.append((hg, a))
-                elif idx == 2:
-                    for third in range(3):
-                        quant_items.append((blk, third))
-            if quant_done < len(quant_items):
-                quant_qk(quant_items[quant_done][0], quant_items[quant_done][1])
-                pair_items.append(quant_items[quant_done])
-                quant_done += 1
             if pair is not None:
                 job = rope_s(pair)
                 if pair[1] not in PE_SUM:
@@ -457,4 +470,4 @@ def tile_windowattention_pa_kernel(tc, x, qkv_w_bytes, qkv_w_scale, qkv_b, out_0
                 if (job[1], job[2]) not in TB_VECTOR:
                     back_out(job)
         assert quant_done == len(quant_items) and pair_done == len(pair_items) and v_done == len(v_items)
-        assert len(pending_v) == 0 and len(pending_g) == 0 and back_pair is None
+        assert len(pending_v) == 0 and back_pair is None

@@ -195,8 +195,8 @@ def tile_windowattention_pa_kernel(tc, x, qkv_w_bytes, qkv_w_scale, qkv_b, out_0
             for c0 in range(0, K, step):
                 for r2 in range(2):
                     nc.vector.tensor_tensor(
-                        out=wb[:, r2, c0 : c0 + step], in0=b_[:, r2, c0 : c0 + step].bitcast(FP8),
-                        in1=sbc[:, c0 : c0 + step], op=ALU.mult,
+                        out=wb[:, r2, c0 : c0 + step], in0=sbc[:, c0 : c0 + step],
+                        in1=b_[:, r2, c0 : c0 + step].bitcast(FP8), op=ALU.mult,
                     )
             st_wb[i] = wb
 

@@ -20,54 +20,45 @@ PASSES = 3
 NWIN = 4
 HEADS = 32
 HD = 48
+RT = 3
+UH = 8
+UCOLS = RT * P
 JROWS = HEADS * HD
-HB = 16
-BROWS = HB * HD
 SCALE = HD ** -0.5
 OMEGA = [10000.0 ** (-i / 8.0) for i in range(8)]
 
 FLOPS = 2 * 512 * 4608 * 1536
-PE_SUM = (1, 2)
-TB_VECTOR = ((0, 0), (0, 1))
-V_BANKS_SLOT = 4
-
-
-def pos_view(ap, third, pos):
-    if third == 0:
-        return ap.rearrange("p (a z y) -> p a z y", a=4, z=2)[:, :, pos, :]
-    if third == 1:
-        return ap.rearrange("p (az r y) -> p az r y", az=8, r=8)[:, :, pos, :]
-    return ap.rearrange("p (a zr wh win) -> p a zr wh win", a=4, zr=16, wh=2)[:, pos % 4, :, pos // 4, :]
+ORDER = ((0, 0), (0, 1), (2, 0), (0, 2), (0, 3), (2, 1), (1, 0), (1, 1), (2, 2), (1, 2), (1, 3), (2, 3))
 
 
 def tile_windowattention_pa_kernel(tc, x, qkv_w_bytes, qkv_w_scale, qkv_b, out_0, out_1, out_2):
     nc = tc.nc
     outs = [out_0, out_1, out_2]
+    n_units = len(ORDER)
 
     with ExitStack() as ctx:
         const = ctx.enter_context(tc.tile_pool(name="const", bufs=1))
         work = ctx.enter_context(tc.tile_pool(name="work", bufs=2))
         ps_tp = ctx.enter_context(tc.psum_pool(name="ps_tp", bufs=4))
-        ps_mm = ctx.enter_context(tc.psum_pool(name="ps_mm", bufs=4))
+        ps_mm = ctx.enter_context(tc.psum_pool(name="ps_mm", bufs=2))
+        ps_tb = ctx.enter_context(tc.psum_pool(name="ps_tb", bufs=2))
         ctx.enter_context(tc.manual_schedule())
 
-        w_blk = [qkv_w_bytes[b * BROWS : (b + 1) * BROWS, :].rearrange("(p r) k -> p r k", r=6) for b in range(4)]
-        w_v = qkv_w_bytes[2 * JROWS :, :].rearrange("(c p) k -> p c k", p=P)
-
-        units = []
-        for blk in range(4):
-            for idx in range(3):
-                units.append(("qk", blk, idx))
-        for c in range(6):
-            units.append(("v", 4, c))
-        n_units = len(units)
         st_bytes = {}
+        w_rows = qkv_w_bytes.rearrange("(t p) k -> p t k", p=P)
+
+        def first_tile(i):
+            j, un = ORDER[i]
+            return (JROWS // P) * j + RT * un
 
         def load(i):
-            kind, blk, idx = units[i]
-            src = w_blk[blk] if kind == "qk" else w_v
-            b_ = work.tile([P, 2, K], U8, name="wbytes", tag="wbytes", bufs=4)
-            nc.sync.dma_start(out=b_[:], in_=src[:, 2 * idx : 2 * idx + 2, :])
+            b_ = work.tile([P, RT, K], U8, name="wbytes", tag="wbytes", bufs=4)
+            t0 = first_tile(i)
+            if i == 0:
+                for r in range(RT):
+                    nc.sync.dma_start(out=b_[:, r, :], in_=w_rows[:, t0 + r, :])
+            else:
+                nc.sync.dma_start(out=b_[:], in_=w_rows[:, t0 : t0 + RT, :])
             st_bytes[i] = b_
 
         ident_f = const.tile([P, P], F32, name="ident_f")
@@ -76,100 +67,99 @@ def tile_windowattention_pa_kernel(tc, x, qkv_w_bytes, qkv_w_scale, qkv_b, out_0
         make_identity(nc, ident_b[:])
 
         load(0)
-        sbc = const.tile([P, K], F32, name="sbc")
-        srow = qkv_w_scale.rearrange("o k -> (o k)")
-        for g in range(PASSES):
-            nc.sync.dma_start(out=sbc[:, 512 * g : 512 * (g + 1)], in_=srow[512 * g : 512 * (g + 1)].partition_broadcast(P))
-        load(1)
-        x_all = work.tile([P, NWIN, K], BF16, name="x_all", tag="stg", bufs=3, align_bytes=64)
-        gx_all = work.tile([P, 2, 2048], BF16, name="gx_all", tag="stg", bufs=3, align_bytes=64)
+        scale = const.tile([P, PASSES, 4], F32, name="scale")
+        nc.sync.dma_start(out=scale[:], in_=qkv_w_scale.rearrange("o (g p t) -> p (o g) t", p=P, t=4))
+        rb0 = const.tile([P, P], BF16, name="rb0")
+        nc.vector.memset(rb0[:], 0.0)
+        nc.sync.dma_start(out=rb0[0:24, :], in_=qkv_b[0 : 2 * JROWS].rearrange("(t p) -> t p", p=P))
+        x_all = const.tile([P, NWIN, K], BF16, name="x_all")
         for w in range(NWIN):
             nc.sync.dma_start(out=x_all[:, w, :], in_=x[w])
+        load(1)
         load(2)
-
-        rb0 = const.tile([P, P], BF16, name="rb0")
-        rb = const.tile([P, P], BF16, name="rb")
-        nc.vector.memset(rb0[:], 0.0)
-        for blk in range(4):
-            nc.gpsimd.dma_start(
-                out=rb0[6 * blk : 6 * blk + 6, :].rearrange("t (h i) -> t h i", i=8),
-                in_=qkv_b[blk * BROWS : (blk + 1) * BROWS].rearrange("(h t i) -> t h i", t=6, i=8),
-            )
         bias_v = const.tile([P, HEADS, HD], BF16, name="bias_v")
 
-        onehot = const.tile([P, 8], F32, name="onehot")
-        nc.vector.tensor_reduce(out=onehot[:], in_=ident_f[:].rearrange("p (c y) -> p c y", y=HB), axis=AX.X, op=ALU.add)
+        warm = const.tile([P, 1], F32, name="warm")
+        nc.vector.memset(warm[:], 0.0)
+        nc.scalar.activation(out=warm[:], in_=warm[:], func=ACT.Sin)
         posrow = const.tile([P, 8], F32, name="posrow")
         for pos in range(8):
             nc.gpsimd.memset(posrow[:, pos : pos + 1], float(pos))
-        omega = const.tile([P, 8], F32, name="omega")
-        angle = const.tile([P, 2, 8], F32, name="angle")
-        wrap = const.tile([P, 2, 8], F32, name="wrap")
-        trig = const.tile([P, 2, 8], F32, name="trig")
-        cos_s = const.tile([P, 2, 8], F32, name="cos_s")
-        sin_s = const.tile([P, 2, 2, 8], F32, name="sin_s")
+        perm = const.tile([P, P], F32, name="perm")
+        idv = ident_f[:].rearrange("p (b hf i) -> p b hf i", hf=2, i=8)
+        pmv = perm[:].rearrange("p (b hf i) -> p b hf i", hf=2, i=8)
+        for hf in range(2):
+            nc.vector.tensor_copy(out=pmv[:, :, hf, :], in_=idv[:, :, 1 - hf, :])
+        oh16 = const.tile([P, 16], F32, name="oh16")
+        nc.vector.tensor_reduce(out=oh16[:], in_=ident_f[:].rearrange("p (b y) -> p y b", y=16), axis=AX.X, op=ALU.add)
+        ohg = const.tile([P, 8], F32, name="ohg")
+        nc.vector.tensor_reduce(out=ohg[:], in_=ident_f[:].rearrange("p (b y) -> p b y", y=16), axis=AX.X, op=ALU.add)
+        oh8 = const.tile([P, 8], F32, name="oh8")
+        nc.vector.tensor_tensor(out=oh8[:], in0=oh16[:, 0:8], in1=oh16[:, 8:16], op=ALU.add)
+        low = const.tile([P, 1], F32, name="low")
+        nc.vector.tensor_reduce(out=low[:], in_=oh16[:, 0:8], axis=AX.X, op=ALU.add)
+        m3 = const.tile([P, 3], F32, name="m3")
+        for j in range(3):
+            nc.vector.tensor_reduce(out=m3[:, j : j + 1], in_=ohg[:, j:8:3], axis=AX.X, op=ALU.add)
+        sgn = const.tile([P, 1], F32, name="sgn")
+        nc.vector.tensor_scalar(out=sgn[:], in0=low[:], scalar1=2.0, scalar2=-1.0, op0=ALU.mult, op1=ALU.add)
+        om8 = const.tile([P, 8], F32, name="om8")
+        for i in range(8):
+            nc.vector.tensor_scalar(out=om8[:, i : i + 1], in0=oh8[:, i : i + 1], scalar1=OMEGA[i], scalar2=None, op0=ALU.mult)
+        omega = const.tile([P, 1], F32, name="omega")
+        nc.vector.tensor_reduce(out=omega[:], in_=om8[:], axis=AX.X, op=ALU.add)
+        mo = const.tile([P, 3], F32, name="mo")
+        nc.vector.tensor_scalar(out=mo[:], in0=m3[:], scalar1=omega[:], scalar2=None, op0=ALU.mult)
+        angle = const.tile([P, 2, 3, 8], F32, name="angle")
+        for j in range(3):
+            nc.vector.tensor_scalar(
+                out=angle[:, 0, j, :], in0=posrow[:], scalar1=mo[:, j : j + 1], scalar2=math.pi / 2, op0=ALU.mult, op1=ALU.add
+            )
+            nc.vector.tensor_scalar(out=angle[:, 1, j, :], in0=posrow[:], scalar1=mo[:, j : j + 1], scalar2=None, op0=ALU.mult)
+        wrap = const.tile([P, 2, 3, 8], F32, name="wrap")
+        nc.vector.tensor_scalar(out=wrap[:], in0=angle[:], scalar1=math.pi, scalar2=-2.0 * math.pi, op0=ALU.is_gt, op1=ALU.mult)
+        nc.vector.tensor_tensor(out=wrap[:], in0=wrap[:], in1=angle[:], op=ALU.add)
+        trig = const.tile([P, 2, 3, 8], F32, name="trig")
+        cos_t = []
+        sin_t = []
+        for c in range(RT):
+            ct = const.tile([P, 512], F32, name="cos%d" % c)
+            cos_t.append(ct)
+            st = const.tile([P, 512], F32, name="sin%d" % c)
+            sin_t.append(st)
+        zr = const.tile([P, 2, 3, 16], F32, name="zr")
+        tab = const.tile([P, 2, 3, 128], F32, name="tab")
 
         def trig_tables():
-            nc.scalar.activation(out=omega[:, 0:1], in_=onehot[:, 0:1], func=ACT.Copy, scale=OMEGA[0])
-            for c in range(1, 8):
-                nc.scalar.activation(
-                    out=omega[:, c : c + 1], in_=onehot[:, c : c + 1], func=ACT.Identity, scale=OMEGA[c],
-                    bias=omega[:, c - 1 : c],
-                )
-            nc.vector.tensor_scalar(
-                out=angle[:, 0, :], in0=posrow[:], scalar1=omega[:, 7:8], scalar2=math.pi / 2, op0=ALU.mult, op1=ALU.add
-            )
-            nc.vector.tensor_scalar(out=angle[:, 1, :], in0=posrow[:], scalar1=omega[:, 7:8], scalar2=None, op0=ALU.mult)
-            nc.vector.tensor_scalar(
-                out=wrap[:], in0=angle[:], scalar1=math.pi, scalar2=-2.0 * math.pi, op0=ALU.is_gt, op1=ALU.mult
-            )
-            nc.vector.tensor_tensor(out=wrap[:], in0=wrap[:], in1=angle[:], op=ALU.add)
-            nc.scalar.activation(out=trig[:], in_=wrap[:], func=ACT.Sin)
-            for j in range(2):
-                sc = SCALE if j == 0 else 1.0
-                nc.scalar.activation(out=cos_s[:, j], in_=trig[:, 0], func=ACT.Copy, scale=sc)
-                nc.scalar.activation(out=sin_s[:, j, 0], in_=trig[:, 1], func=ACT.Copy, scale=-sc)
-                nc.scalar.activation(out=sin_s[:, j, 1], in_=trig[:, 1], func=ACT.Copy, scale=sc)
-
-        tsin = {}
-        for third in PE_SUM:
-            for half in range(2):
-                ts_ = const.tile([P, 512], F32, name="tsin%d_%d" % (third, half))
-                nc.gpsimd.memset(pos_view(ts_[:], third, 0), 0.0)
-                tsin[(third, half)] = ts_
+            nc.vector.tensor_scalar(out=trig[:, 1], in0=trig[:, 1], scalar1=sgn[:], scalar2=None, op0=ALU.mult)
+            for c in range(RT):
+                for s_, op in ((0, ALU.mult), (1, ALU.add)):
+                    tz, tr, tw = (trig[:, s_, (third + c) % 3, :] for third in range(3))
+                    nc.vector.tensor_tensor(
+                        out=zr[:, s_, c, :].rearrange("p (z r) -> p z r", z=2),
+                        in0=tz[:, 0:2].unsqueeze(2).to_broadcast([P, 2, 8]),
+                        in1=tr.unsqueeze(1).to_broadcast([P, 2, 8]), op=op,
+                    )
+                    nc.vector.tensor_tensor(
+                        out=tab[:, s_, c, :].rearrange("p (a zr wh) -> p zr wh a", a=4, zr=16),
+                        in0=zr[:, s_, c, :].unsqueeze(2).unsqueeze(3).to_broadcast([P, 16, 2, 4]),
+                        in1=tw.rearrange("p (wh a) -> p wh a", wh=2).unsqueeze(1).to_broadcast([P, 16, 2, 4]), op=op,
+                    )
+            for c in range(RT):
+                for s_, full in ((0, cos_t[c]), (1, sin_t[c])):
+                    nc.vector.tensor_copy(
+                        out=full[:].rearrange("p (n w) -> p n w", w=NWIN),
+                        in_=tab[:, s_, c, :].unsqueeze(2).to_broadcast([P, 128, NWIN]),
+                    )
 
         bt = const.tile([P, 24], F32, name="bt")
-        btab = const.tile([P, 24, 8], F32, name="btab")
-        tmpb = const.tile([P, 24, 8], F32, name="tmpb")
-
-        def bias_tables():
-            nc.vector.tensor_copy(out=rb[:].rearrange("p (i h) -> p i h", h=HB), in_=rb0[:].rearrange("p (h i) -> p i h", i=8))
-            bps = ps_tp.tile([P, 512], F32, name="bps", tag="tp")
-            nc.tensor.matmul(out=bps[:, 0:24], lhsT=rb[:], rhs=ident_b[:, 0:24], start=True, stop=True)
-            nc.vector.tensor_copy(out=bt[:], in_=bps[:, 0:24])
-            for j in range(2):
-                btj = bt[:, 12 * j : 12 * j + 12]
-                nc.vector.tensor_tensor(
-                    out=btab[:, 12 * j : 12 * j + 12, :],
-                    in0=cos_s[:, j].unsqueeze(1).to_broadcast([P, 12, 8]),
-                    in1=btj.unsqueeze(2).to_broadcast([P, 12, 8]),
-                    op=ALU.mult,
-                )
-                for half in range(2):
-                    nc.vector.tensor_tensor(
-                        out=tmpb[:, 12 * j : 12 * j + 12, :].rearrange("p (q hf) pos -> p q hf pos", hf=2)[:, :, half],
-                        in0=sin_s[:, j, half].unsqueeze(1).to_broadcast([P, 6, 8]),
-                        in1=btj.rearrange("p (q hf) -> p q hf", hf=2)[:, :, 1 - half].unsqueeze(2).to_broadcast([P, 6, 8]),
-                        op=ALU.mult,
-                    )
-            nc.vector.tensor_tensor(out=btab[:], in0=btab[:], in1=tmpb[:], op=ALU.add)
 
         xcodes = const.tile([P, PASSES, 512], U32, name="xcodes", align_bytes=64)
         xplanes = const.tile([P, PASSES, 512], U8, name="xplanes", align_bytes=64)
+        gx_all = const.tile([P, PASSES, 2048], BF16, name="gx_all", align_bytes=64)
 
         def x_pass(g):
-            gx = gx_all[:, g % 2, :]
-            gxw = gx.bitcast(F32).rearrange("p (a m wp y) -> p wp a m y", a=4, m=32, wp=2)
+            gxw = gx_all[:, g, :].bitcast(F32).rearrange("p (a m wp y) -> p wp a m y", a=4, m=32, wp=2)
             for wp in range(2):
                 wt = ps_tp.tile([P, 4, P], F32, name="wt", tag="tp")
                 for win2 in range(2):
@@ -181,80 +171,65 @@ def tile_windowattention_pa_kernel(tc, x, qkv_w_bytes, qkv_w_scale, qkv_b, out_0
                 nc.scalar.copy(out=gxw[:, wp], in_=wt[:].rearrange("p y (m a) -> p a m y", a=4))
 
         def x_quant(g):
-            nc.vector.quantize_mx(out=xcodes[:, g, :].bitcast(FP8X4), scales=xplanes[:, g, :], in_=gx_all[:, g % 2, :])
+            nc.vector.quantize_mx(out=xcodes[:, g, :].bitcast(FP8X4), scales=xplanes[:, g, :], in_=gx_all[:, g, :])
 
         st_wb = {}
         st_g = {}
         st_codes = {}
-        o_qk = {}
+        st_prod = {}
+        st_out = {}
 
-        def widen(i):
-            b_ = st_bytes[i]
-            wb = work.tile([P, 2, K], BF16, name="wb", tag="wb", bufs=3)
-            step = 512 if i == 0 else K
-            for c0 in range(0, K, step):
-                for r2 in range(2):
-                    nc.vector.tensor_tensor(
-                        out=wb[:, r2, c0 : c0 + step], in0=sbc[:, c0 : c0 + step],
-                        in1=b_[:, r2, c0 : c0 + step].bitcast(FP8), op=ALU.mult,
-                    )
+        def cast(i):
+            wb = work.tile([P, RT, K], BF16, name="wb", tag="wb", bufs=3)
+            for r in range(RT):
+                nc.scalar.copy(out=wb[:, r, :], in_=st_bytes[i][:, r, :].bitcast(FP8))
             st_wb[i] = wb
 
-        def turn(i):
-            kind, blk, idx = units[i]
-            wb = st_wb[i]
-            if kind == "v" or idx == 0:
-                grp_new = work.tile([P, PASSES, 3072], BF16, name="grp", tag="grp", bufs=2, align_bytes=64)
-                st_g[(blk, idx if kind == "v" else 0)] = grp_new
-            grp = st_g[(blk, idx if kind == "v" else 0)]
-            for g in range(PASSES):
-                wt = ps_tp.tile([P, 4, P], F32, name="wt", tag="tp")
-                for r2 in range(2):
-                    words = wb[:, r2, :].bitcast(F32)
-                    for u in range(2):
-                        nc.tensor.transpose(
-                            wt[:, 2 * r2 + u, :], words[:, 256 * g + u : 256 * (g + 1) : 2], ident_f[:]
-                        )
-                if kind == "qk":
-                    gw = grp[:, g, :].bitcast(F32).rearrange("p (c8 r h u) -> p r c8 h u", c8=8, r=6, h=HB)
-                    for r2 in range(2):
-                        nc.scalar.copy(
-                            out=gw[:, 2 * idx + r2],
-                            in_=wt[:, 2 * r2 : 2 * r2 + 2, :].rearrange("p u (h c8) -> p c8 h u", c8=8),
-                        )
-                else:
-                    gw = grp[:, g, 0:1024].bitcast(F32)
-                    nc.scalar.copy(
-                        out=gw.rearrange("p (c2 col u) -> p c2 col u", c2=2, u=2),
-                        in_=wt[:].rearrange("p (c2 u) col -> p c2 col u", u=2),
+        def t_pair(i, g):
+            wt = ps_tp.tile([P, 2, 2 * P], F32, name="wt2", tag="tp")
+            for r in range(2):
+                words = st_wb[i][:, r, :].bitcast(F32)
+                for u in range(2):
+                    nc.tensor.transpose(
+                        wt[:, u, r * P : (r + 1) * P], words[:, 256 * g + u : 256 * (g + 1) : 2], ident_f[:]
                     )
+            return [(wt[:], g, 0, 2 * P)]
 
-        def quant_qk(blk, third):
-            if third == 0:
-                codes_new = work.tile([P, PASSES, 768], U32, name="codes", tag="codes", bufs=2, align_bytes=64)
-                planes_new = work.tile([P, PASSES, 768], U8, name="planes", tag="planes", bufs=2, align_bytes=64)
-                st_codes[blk] = (codes_new, planes_new)
-            codes, planes = st_codes[blk]
-            grp = st_g[(blk, 0)]
-            cols = slice(256 * third, 256 * (third + 1))
-            for g in range(PASSES):
+        def t_third(i, gs):
+            wt = ps_tp.tile([P, 2, 2, P], F32, name="wt3", tag="tp")
+            words = st_wb[i][:, 2, :].bitcast(F32)
+            jobs = []
+            for gi, g in enumerate(gs):
+                for u in range(2):
+                    nc.tensor.transpose(wt[:, gi, u, :], words[:, 256 * g + u : 256 * (g + 1) : 2], ident_f[:])
+                jobs.append((wt[:, gi], g, 2 * P, P))
+            return jobs
+
+        def scaled_out(i, job):
+            src, g, col0, cols = job
+            nc.vector.tensor_tensor(
+                out=st_g[i][:, g, 4 * col0 : 4 * (col0 + cols)].rearrange("p (c u e) -> p c u e", u=2, e=2),
+                in0=src.rearrange("p u c -> p (u c)").bitcast(BF16).rearrange("p (u c e) -> p c u e", u=2, e=2),
+                in1=scale[:, g, :].rearrange("p (u e) -> p u e", e=2).unsqueeze(1).to_broadcast([P, cols, 2, 2]),
+                op=ALU.mult,
+            )
+
+        def quant(i):
+            codes = work.tile([P, PASSES, UCOLS], U32, name="codes", tag="codes", bufs=2, align_bytes=64)
+            planes = work.tile([P, PASSES, UCOLS], U8, name="planes", tag="planes", bufs=2, align_bytes=64)
+            cf = codes[:].rearrange("p g c -> p (g c)")
+            pf = planes[:].rearrange("p g c -> p (g c)")
+            gf = st_g[i][:].rearrange("p g c -> p (g c)")
+            for c0, cn in ((0, 1024), (1024, 128)):
                 nc.vector.quantize_mx(
-                    out=codes[:, g, cols].bitcast(FP8X4), scales=planes[:, g, cols],
-                    in_=grp[:, g, 1024 * third : 1024 * (third + 1)],
+                    out=cf[:, c0 : c0 + cn].bitcast(FP8X4), scales=pf[:, c0 : c0 + cn], in_=gf[:, 4 * c0 : 4 * (c0 + cn)]
                 )
+            st_codes[i] = (codes, planes)
 
-        def quant_v(c):
-            grp = st_g[(4, c)]
-            codes = work.tile([P, PASSES, 256], U32, name="vcodes", tag="vcodes", bufs=4, align_bytes=64)
-            planes = work.tile([P, PASSES, 256], U8, name="vplanes", tag="vplanes", bufs=4, align_bytes=64)
-            for g in range(PASSES):
-                nc.vector.quantize_mx(out=codes[:, g, :].bitcast(FP8X4), scales=planes[:, g, :], in_=grp[:, g, 0:1024])
-            st_codes[(4, c)] = (codes, planes)
-
-        def mx(blk, tile_no):
-            codes, planes = st_codes[blk]
+        def mx_tile(i, c):
+            codes, planes = st_codes[i]
             mm = ps_mm.tile([P, 512], F32, name="mm", tag="mm")
-            cols = slice(tile_no * P, (tile_no + 1) * P)
+            cols = slice(c * P, (c + 1) * P)
             for g in range(PASSES):
                 nc.tensor.matmul_mx(
                     out=mm[:],
@@ -264,210 +239,121 @@ def tile_windowattention_pa_kernel(tc, x, qkv_w_bytes, qkv_w_scale, qkv_b, out_0
                 )
             return mm
 
-        def pair_mx(blk, third):
-            return (blk, third, mx(blk, 2 * third), mx(blk, 2 * third + 1))
+        def biased(i, c, mm):
+            j = ORDER[i][0]
+            y = work.tile([P, 512], F32, name="y", tag="y", bufs=4)
+            col = first_tile(i) + c
+            nc.scalar.activation(
+                out=y[:], in_=mm[:], func=ACT.Identity, scale=SCALE if j == 0 else 1.0, bias=bt[:, col : col + 1]
+            )
+            return y
 
-        def rope_s(pair):
-            blk, third, mm_lo, mm_hi = pair
-            j = blk // 2
-            npos = 2 if third == 0 else 8
-            jobs = []
-            for half, own, other in ((0, mm_lo, mm_hi), (1, mm_hi, mm_lo)):
-                col = 6 * blk + 2 * third + half
-                o_ = work.tile([P, 512], F32, name="o", tag="o", bufs=4)
-                o_qk[(blk, third, half)] = o_
-                if third in PE_SUM:
-                    for pos in range(npos):
-                        nc.scalar.activation(
-                            out=pos_view(o_[:], third, pos), in_=pos_view(own[:], third, pos), func=ACT.Identity,
-                            scale=cos_s[:, j, pos : pos + 1], bias=btab[:, col, pos : pos + 1],
-                        )
-                    for pos in range(1, npos):
-                        nc.scalar.activation(
-                            out=pos_view(tsin[(third, half)][:], third, pos), in_=pos_view(other[:], third, pos),
-                            func=ACT.Copy, scale=sin_s[:, j, half, pos : pos + 1],
-                        )
-                    continue
-                t_ = work.tile([P, 512], F32, name="t", tag="t", bufs=2)
-                nc.scalar.activation(
-                    out=pos_view(o_[:], third, 0), in_=pos_view(own[:], third, 0), func=ACT.Identity,
-                    scale=cos_s[:, j, 0:1], bias=btab[:, col, 0:1],
+        def products(i, c, y):
+            ya = work.tile([P, 512], F32, name="ya", tag="ya", bufs=6)
+            nc.gpsimd.tensor_tensor(out=ya[:], in0=y[:], in1=cos_t[c][:], op=ALU.mult)
+            yb = work.tile([P, 512], F32, name="yb", tag="yb", bufs=6)
+            nc.gpsimd.tensor_tensor(out=yb[:], in0=y[:], in1=sin_t[c][:], op=ALU.mult)
+            st_prod[(i, c)] = (ya, yb)
+
+        def back_t(i, a):
+            tb = ps_tb.tile([P, UCOLS], F32, name="tb", tag="tb")
+            toks = slice(a * P, (a + 1) * P)
+            for c in range(RT):
+                ya, yb = st_prod[(i, c)]
+                dst = tb[:, c * P : (c + 1) * P]
+                nc.tensor.matmul(out=dst, lhsT=ya[:, toks], rhs=ident_f[:], is_transpose=True, start=True, stop=False)
+                nc.tensor.matmul(out=dst, lhsT=yb[:, toks], rhs=perm[:], is_transpose=True, start=False, stop=True)
+            return tb
+
+        def store(i, stg):
+            j, un = ORDER[i]
+            for win in range(NWIN):
+                nc.sync.dma_start(
+                    out=outs[j][win, UH * un : UH * (un + 1)].rearrange("h (m a) e -> m h (a e)", a=4),
+                    in_=stg[win : P : 4, :, :, :].rearrange("p h a e -> p h (a e)"),
                 )
-                for pos in range(1, npos):
-                    nc.scalar.activation(
-                        out=pos_view(t_[:], third, pos), in_=pos_view(other[:], third, pos), func=ACT.Identity,
-                        scale=sin_s[:, j, half, pos : pos + 1], bias=btab[:, col, pos : pos + 1],
-                    )
-                jobs.append((o_, t_, own))
-            return (j, third, npos, jobs)
 
-        def rope_v(job):
-            j, third, npos, jobs = job
-            for o_, t_, own in jobs:
-                for pos in range(1, npos):
-                    nc.vector.scalar_tensor_tensor(
-                        out=pos_view(o_[:], third, pos), in0=pos_view(own[:], third, pos),
-                        scalar=cos_s[:, j, pos : pos + 1], in1=pos_view(t_[:], third, pos),
-                        op0=ALU.mult, op1=ALU.add,
-                    )
-
-        stg_tiles = {}
-
-        def back_t(blk, third, ah):
-            tb = ps_tp.tile([P, 2, 2, P], F32, name="tb", tag="tp")
-            for a2 in range(2):
-                toks = slice((2 * ah + a2) * P, (2 * ah + a2 + 1) * P)
-                for half in range(2):
-                    if third in PE_SUM:
-                        nc.tensor.matmul(
-                            out=tb[:, a2, half, :], lhsT=o_qk[(blk, third, half)][:, toks], rhs=ident_f[:],
-                            is_transpose=True, start=True, stop=False,
-                        )
-                        nc.tensor.matmul(
-                            out=tb[:, a2, half, :], lhsT=tsin[(third, half)][:, toks], rhs=ident_f[:],
-                            is_transpose=True, start=False, stop=True,
-                        )
-                    else:
-                        nc.tensor.transpose(tb[:, a2, half, :], o_qk[(blk, third, half)][:, toks], ident_f[:])
-            return (blk, third, ah, tb)
-
-        def back_out(job):
-            blk, third, ah, tb = job
-            if third == 0 and ah == 0:
-                stg_new = work.tile([P, HB, 4, HD], F32, name="stg", tag="stg", bufs=3, align_bytes=64)
-                stg_tiles[blk] = stg_new
-            stg = stg_tiles[blk]
-            dst = stg[:, :, 2 * ah : 2 * ah + 2, 16 * third : 16 * third + 16]
-            src = tb[:].rearrange("p a2 hf (i h) -> p h a2 (hf i)", h=HB)
-            if (third, ah) in TB_VECTOR:
-                nc.vector.tensor_copy(out=dst, in_=src)
-            else:
-                nc.scalar.copy(out=dst, in_=src)
-            if third == 2 and ah == 1:
-                j, hh = blk // 2, blk % 2
-                for win in range(NWIN):
-                    nc.sync.dma_start(
-                        out=outs[j][win, HB * hh : HB * (hh + 1)].rearrange("h (m a) e -> m h (a e)", a=4),
-                        in_=stg[win : P : 4, :, :, :].rearrange("p h a e -> p h (a e)"),
-                    )
-
-        sv_tiles = {}
-
-        def v_bank(hg, a):
+        def back_out(i, a, tb):
             if a == 0:
-                sv_new = work.tile([P, 8, 4, HD], F32, name="sv", tag="sv", bufs=4)
-                sv_tiles[hg] = sv_new
+                stg_new = work.tile([P, UH, 4, HD], F32, name="stg", tag="stg", bufs=3)
+                st_out[i] = stg_new
+            nc.scalar.copy(out=st_out[i][:, :, a, :], in_=tb[:].rearrange("p (h e) -> p h e", e=HD))
+            if a == 3:
+                store(i, st_out[i])
+
+        def v_bank(i, a):
+            codes, planes = st_codes[i]
             mm = ps_mm.tile([P, 512], F32, name="mm", tag="mm")
             toks = slice(a * P, (a + 1) * P)
-            for k3 in range(3):
-                c = 3 * hg + k3
-                codes, planes = st_codes[(4, c // 2)]
-                cols = slice((c % 2) * P, (c % 2 + 1) * P)
+            for c0, cn in ((0, 256), (256, 128)):
                 for g in range(PASSES):
                     nc.tensor.matmul_mx(
-                        out=mm[:, k3 * P : (k3 + 1) * P],
+                        out=mm[:, c0 : c0 + cn],
                         lhsT=xcodes[:, g, toks].bitcast(FP8X4), lhsT_scale=xplanes[:, g, toks],
-                        rhs=codes[:, g, cols].bitcast(FP8X4), rhs_scale=planes[:, g, cols],
+                        rhs=codes[:, g, c0 : c0 + cn].bitcast(FP8X4), rhs_scale=planes[:, g, c0 : c0 + cn],
                         start=(g == 0), stop=(g == PASSES - 1),
                     )
-            return (hg, a, mm)
+            return mm
 
-        def v_bank_out(job):
-            hg, a, mm = job
-            sv = sv_tiles[hg]
+        def v_out(i, a, mm):
+            un = ORDER[i][1]
+            if a == 0:
+                sv_new = work.tile([P, UH, 4, HD], F32, name="sv", tag="sv", bufs=3)
+                st_out[i] = sv_new
             nc.vector.tensor_tensor(
-                out=sv[:, :, a, :], in0=mm[:, 0 : 3 * P].rearrange("p (h e) -> p h e", e=HD),
-                in1=bias_v[:, 8 * hg : 8 * hg + 8, :], op=ALU.add,
+                out=st_out[i][:, :, a, :], in0=mm[:, 0:UCOLS].rearrange("p (h e) -> p h e", e=HD),
+                in1=bias_v[:, UH * un : UH * (un + 1), :], op=ALU.add,
             )
             if a == 3:
-                for win in range(NWIN):
-                    nc.sync.dma_start(
-                        out=outs[2][win, 8 * hg : 8 * hg + 8].rearrange("h (m a) e -> m h (a e)", a=4),
-                        in_=sv[win : P : 4, :, :, :].rearrange("p h a e -> p h (a e)"),
-                    )
+                store(i, st_out[i])
 
-        quant_items = []
-        pair_items = []
-        v_items = []
-        quant_done = 0
-        pair_done = 0
-        v_done = 0
-        back_pair = None
-        fresh_v = []
-        fresh_pairs = []
-        pending_v = []
-        widen(0)
+        cast(0)
+        nc.scalar.activation(out=trig[:], in_=wrap[:], func=ACT.Sin)
         for s in range(n_units + 3):
-            if s + 3 < n_units:
-                load(s + 3)
-            if s < n_units:
-                turn(s)
-            if s < PASSES:
-                x_pass(s)
+            if 1 <= s and s + 2 < n_units:
+                load(s + 2)
             if s + 1 < n_units:
-                widen(s + 1)
-            for job in pending_v:
-                rope_v(job)
-            pending_v = []
-            if s < PASSES:
-                x_quant(s)
-            if s == 1:
+                cast(s + 1)
+            jobs = []
+            if s < n_units:
+                grp = work.tile([P, PASSES, 4 * UCOLS], BF16, name="grp", tag="grp", bufs=2, align_bytes=64)
+                st_g[s] = grp
+                for g in range(PASSES):
+                    jobs.extend(t_pair(s, g))
+                jobs.extend(t_third(s, (0, 1)))
+            prev_v = 1 <= s <= n_units and ORDER[s - 1][0] == 2
+            if 1 <= s <= n_units:
+                if prev_v:
+                    for a in range(4):
+                        mm = v_bank(s - 1, a)
+                        if a < len(jobs):
+                            scaled_out(s, jobs[a])
+                        v_out(s - 1, a, mm)
+                    jobs = jobs[4:]
+                else:
+                    for c in range(RT):
+                        mm = mx_tile(s - 1, c)
+                        y = biased(s - 1, c, mm)
+                        products(s - 1, c, y)
+            for job in jobs:
+                scaled_out(s, job)
+            if s < n_units:
+                for job in t_third(s, (2,)):
+                    scaled_out(s, job)
+                quant(s)
+            if s == 0:
+                for g in range(PASSES):
+                    x_pass(g)
+                bps = ps_tb.tile([P, UCOLS], F32, name="bps", tag="tb")
+                nc.tensor.matmul(out=bps[:, 0:24], lhsT=rb0[:], rhs=ident_b[:, 0:24], start=True, stop=True)
+                for g in range(PASSES):
+                    x_quant(g)
+                nc.vector.tensor_scalar(out=bt[:, 0:12], in0=bps[:, 0:12], scalar1=SCALE, scalar2=None, op0=ALU.mult)
+                nc.vector.tensor_copy(out=bt[:, 12:24], in_=bps[:, 12:24])
                 trig_tables()
-            if s == 2:
-                bias_tables()
-            if s == 4:
                 nc.sync.dma_start(
                     out=bias_v[:].rearrange("p h e -> p (h e)"), in_=qkv_b[2 * JROWS :].partition_broadcast(P)
                 )
-            for item in fresh_v:
-                v_items.append(item)
-            fresh_v = []
-            for item in fresh_pairs:
-                pair_items.append(item)
-            fresh_pairs = []
-            if s < n_units:
-                kind, blk, idx = units[s]
-                if kind == "v":
-                    quant_v(idx)
-                    for hg in range(4):
-                        if (3 * hg + 2) // 2 == idx:
-                            for a in range(4):
-                                fresh_v.append((hg, a))
-                elif idx == 2:
-                    for third in range(3):
-                        quant_items.append((blk, third))
-            if quant_done < len(quant_items):
-                quant_qk(quant_items[quant_done][0], quant_items[quant_done][1])
-                fresh_pairs.append(quant_items[quant_done])
-                quant_done += 1
-            if s == n_units - 1:
-                for item in fresh_v:
-                    v_items.append(item)
-                fresh_v = []
-            banks_left = V_BANKS_SLOT if s < n_units - 1 else 8
-            pair = None
-            if pair_done < len(pair_items):
-                pair = pair_mx(pair_items[pair_done][0], pair_items[pair_done][1])
-                pair_done += 1
-                banks_left -= 2
-            while banks_left > 0 and v_done < len(v_items):
-                v_bank_out(v_bank(v_items[v_done][0], v_items[v_done][1]))
-                v_done += 1
-                banks_left -= 1
-            back_jobs = []
-            if back_pair is not None:
-                back_jobs = [back_t(back_pair[0], back_pair[1], ah) for ah in range(2)]
-            back_pair = None
-            for job in back_jobs:
-                if (job[1], job[2]) in TB_VECTOR:
-                    back_out(job)
-            if pair is not None:
-                job = rope_s(pair)
-                if pair[1] not in PE_SUM:
-                    pending_v.append(job)
-                back_pair = (pair[0], pair[1])
-            for job in back_jobs:
-                if (job[1], job[2]) not in TB_VECTOR:
-                    back_out(job)
-        assert quant_done == len(quant_items) and pair_done == len(pair_items) and v_done == len(v_items)
-        assert len(pending_v) == 0 and back_pair is None
+            if 2 <= s <= n_units + 1 and ORDER[s - 2][0] != 2:
+                for a in range(4):
+                    back_out(s - 2, a, back_t(s - 2, a))

@@ -31,6 +31,14 @@ FLOPS = 2 * 512 * 4608 * 1536
 ORDER = ((0, 0), (0, 1), (2, 0), (0, 2), (0, 3), (2, 1), (1, 0), (1, 1), (2, 2), (1, 2), (1, 3), (2, 3))
 
 
+def pos_view(ap, third, pos):
+    if third == 0:
+        return ap.rearrange("p (a z y) -> p a z y", a=4, z=2)[:, :, pos, :]
+    if third == 1:
+        return ap.rearrange("p (az r y) -> p az r y", az=8, r=8)[:, :, pos, :]
+    return ap.rearrange("p (a zr wh win) -> p a zr wh win", a=4, zr=16, wh=2)[:, pos % 4, :, pos // 4, :]
+
+
 def tile_windowattention_pa_kernel(tc, x, qkv_w_bytes, qkv_w_scale, qkv_b, out_0, out_1, out_2):
     nc = tc.nc
     outs = [out_0, out_1, out_2]
@@ -45,20 +53,13 @@ def tile_windowattention_pa_kernel(tc, x, qkv_w_bytes, qkv_w_scale, qkv_b, out_0
         ctx.enter_context(tc.manual_schedule())
 
         st_bytes = {}
-        w_rows = qkv_w_bytes.rearrange("(t p) k -> p t k", p=P)
-
-        def first_tile(i):
-            j, un = ORDER[i]
-            return (JROWS // P) * j + RT * un
 
         def load(i):
+            j, un = ORDER[i]
+            rows = qkv_w_bytes[JROWS * j + UCOLS * un : JROWS * j + UCOLS * (un + 1), :].rearrange("(p r) k -> p r k", r=RT)
             b_ = work.tile([P, RT, K], U8, name="wbytes", tag="wbytes", bufs=4)
-            t0 = first_tile(i)
-            if i == 0:
-                for r in range(RT):
-                    nc.sync.dma_start(out=b_[:, r, :], in_=w_rows[:, t0 + r, :])
-            else:
-                nc.sync.dma_start(out=b_[:], in_=w_rows[:, t0 : t0 + RT, :])
+            nc.sync.dma_start(out=b_[:, 0, :], in_=rows[:, 0, :])
+            nc.sync.dma_start(out=b_[:, 1:RT, :], in_=rows[:, 1:RT, :])
             st_bytes[i] = b_
 
         ident_f = const.tile([P, P], F32, name="ident_f")
@@ -66,15 +67,19 @@ def tile_windowattention_pa_kernel(tc, x, qkv_w_bytes, qkv_w_scale, qkv_b, out_0
         ident_b = const.tile([P, P], BF16, name="ident_b")
         make_identity(nc, ident_b[:])
 
+        rb0 = const.tile([P, P], BF16, name="rb0")
+        nc.vector.memset(rb0[:], 0.0)
+        for t in range(3):
+            nc.gpsimd.dma_start(
+                out=rb0[8 * t : 8 * t + 8, :].rearrange("u (h e) -> u h e", e=16),
+                in_=qkv_b[0 : 2 * JROWS].rearrange("(u h t e) -> t u h e", u=8, h=UH, e=16)[t],
+            )
         load(0)
         scale = const.tile([P, PASSES, 4], F32, name="scale")
         nc.sync.dma_start(out=scale[:], in_=qkv_w_scale.rearrange("o (g p t) -> p (o g) t", p=P, t=4))
-        rb0 = const.tile([P, P], BF16, name="rb0")
-        nc.vector.memset(rb0[:], 0.0)
-        nc.sync.dma_start(out=rb0[0:24, :], in_=qkv_b[0 : 2 * JROWS].rearrange("(t p) -> t p", p=P))
         x_all = const.tile([P, NWIN, K], BF16, name="x_all")
-        for w in range(NWIN):
-            nc.sync.dma_start(out=x_all[:, w, :], in_=x[w])
+        for w in range(2):
+            nc.sync.dma_start(out=x_all[:, 2 * w : 2 * w + 2, :], in_=x[2 * w : 2 * w + 2].rearrange("w p k -> p w k"))
         load(1)
         load(2)
         bias_v = const.tile([P, HEADS, HD], BF16, name="bias_v")
@@ -84,75 +89,64 @@ def tile_windowattention_pa_kernel(tc, x, qkv_w_bytes, qkv_w_scale, qkv_b, out_0
         nc.scalar.activation(out=warm[:], in_=warm[:], func=ACT.Sin)
         posrow = const.tile([P, 8], F32, name="posrow")
         for pos in range(8):
-            nc.gpsimd.memset(posrow[:, pos : pos + 1], float(pos))
-        perm = const.tile([P, P], F32, name="perm")
-        idv = ident_f[:].rearrange("p (b hf i) -> p b hf i", hf=2, i=8)
-        pmv = perm[:].rearrange("p (b hf i) -> p b hf i", hf=2, i=8)
+            nc.vector.memset(posrow[:, pos : pos + 1], float(pos))
+        sort_p = const.tile([P, P], F32, name="sort_p")
+        nc.vector.tensor_copy(
+            out=sort_p[:].rearrange("p (c h) -> p c h", h=UH), in_=ident_f[:].rearrange("p (h c) -> p c h", h=UH)
+        )
+        swap_p = const.tile([P, P], F32, name="swap_p")
         for hf in range(2):
-            nc.vector.tensor_copy(out=pmv[:, :, hf, :], in_=idv[:, :, 1 - hf, :])
+            nc.vector.tensor_copy(out=swap_p[:, 64 * hf : 64 * hf + 64], in_=ident_f[:, 64 - 64 * hf : 128 - 64 * hf])
         oh16 = const.tile([P, 16], F32, name="oh16")
-        nc.vector.tensor_reduce(out=oh16[:], in_=ident_f[:].rearrange("p (b y) -> p y b", y=16), axis=AX.X, op=ALU.add)
-        ohg = const.tile([P, 8], F32, name="ohg")
-        nc.vector.tensor_reduce(out=ohg[:], in_=ident_f[:].rearrange("p (b y) -> p b y", y=16), axis=AX.X, op=ALU.add)
+        nc.vector.tensor_reduce(out=oh16[:], in_=ident_f[:].rearrange("p (b y) -> p b y", y=8), axis=AX.X, op=ALU.add)
         oh8 = const.tile([P, 8], F32, name="oh8")
         nc.vector.tensor_tensor(out=oh8[:], in0=oh16[:, 0:8], in1=oh16[:, 8:16], op=ALU.add)
         low = const.tile([P, 1], F32, name="low")
         nc.vector.tensor_reduce(out=low[:], in_=oh16[:, 0:8], axis=AX.X, op=ALU.add)
-        m3 = const.tile([P, 3], F32, name="m3")
-        for j in range(3):
-            nc.vector.tensor_reduce(out=m3[:, j : j + 1], in_=ohg[:, j:8:3], axis=AX.X, op=ALU.add)
-        sgn = const.tile([P, 1], F32, name="sgn")
-        nc.vector.tensor_scalar(out=sgn[:], in0=low[:], scalar1=2.0, scalar2=-1.0, op0=ALU.mult, op1=ALU.add)
         om8 = const.tile([P, 8], F32, name="om8")
         for i in range(8):
             nc.vector.tensor_scalar(out=om8[:, i : i + 1], in0=oh8[:, i : i + 1], scalar1=OMEGA[i], scalar2=None, op0=ALU.mult)
+        sgn = const.tile([P, 1], F32, name="sgn")
+        nc.vector.tensor_scalar(out=sgn[:], in0=low[:], scalar1=2.0, scalar2=-1.0, op0=ALU.mult, op1=ALU.add)
         omega = const.tile([P, 1], F32, name="omega")
         nc.vector.tensor_reduce(out=omega[:], in_=om8[:], axis=AX.X, op=ALU.add)
-        mo = const.tile([P, 3], F32, name="mo")
-        nc.vector.tensor_scalar(out=mo[:], in0=m3[:], scalar1=omega[:], scalar2=None, op0=ALU.mult)
-        angle = const.tile([P, 2, 3, 8], F32, name="angle")
-        for j in range(3):
-            nc.vector.tensor_scalar(
-                out=angle[:, 0, j, :], in0=posrow[:], scalar1=mo[:, j : j + 1], scalar2=math.pi / 2, op0=ALU.mult, op1=ALU.add
-            )
-            nc.vector.tensor_scalar(out=angle[:, 1, j, :], in0=posrow[:], scalar1=mo[:, j : j + 1], scalar2=None, op0=ALU.mult)
-        wrap = const.tile([P, 2, 3, 8], F32, name="wrap")
+        angle = const.tile([P, 2, 8], F32, name="angle")
+        nc.vector.tensor_scalar(
+            out=angle[:, 0, :], in0=posrow[:], scalar1=omega[:], scalar2=math.pi / 2, op0=ALU.mult, op1=ALU.add
+        )
+        nc.vector.tensor_scalar(out=angle[:, 1, :], in0=posrow[:], scalar1=omega[:], scalar2=None, op0=ALU.mult)
+        wrap = const.tile([P, 2, 8], F32, name="wrap")
         nc.vector.tensor_scalar(out=wrap[:], in0=angle[:], scalar1=math.pi, scalar2=-2.0 * math.pi, op0=ALU.is_gt, op1=ALU.mult)
         nc.vector.tensor_tensor(out=wrap[:], in0=wrap[:], in1=angle[:], op=ALU.add)
-        trig = const.tile([P, 2, 3, 8], F32, name="trig")
-        cos_t = []
-        sin_t = []
-        for c in range(RT):
-            ct = const.tile([P, 512], F32, name="cos%d" % c)
-            cos_t.append(ct)
-            st = const.tile([P, 512], F32, name="sin%d" % c)
-            sin_t.append(st)
-        zr = const.tile([P, 2, 3, 16], F32, name="zr")
-        tab = const.tile([P, 2, 3, 128], F32, name="tab")
+        trig = const.tile([P, 2, 8], F32, name="trig")
+        cs = const.tile([P, 2, 2, 8], F32, name="cs")
+        bt = const.tile([P, 3, 8], F32, name="bt")
+        bcs = const.tile([P, 2, 3, 8, 8], F32, name="bcs")
+        rb = const.tile([P, P], BF16, name="rb")
 
         def trig_tables():
-            nc.vector.tensor_scalar(out=trig[:, 1], in0=trig[:, 1], scalar1=sgn[:], scalar2=None, op0=ALU.mult)
-            for c in range(RT):
-                for s_, op in ((0, ALU.mult), (1, ALU.add)):
-                    tz, tr, tw = (trig[:, s_, (third + c) % 3, :] for third in range(3))
+            for j in range(2):
+                sc = SCALE if j == 0 else 1.0
+                nc.vector.tensor_scalar(out=cs[:, j, 0, :], in0=trig[:, 0, :], scalar1=sc, scalar2=None, op0=ALU.mult)
+                nc.vector.tensor_scalar(out=cs[:, j, 1, :], in0=trig[:, 1, :], scalar1=sgn[:], scalar2=sc, op0=ALU.mult, op1=ALU.mult)
+            nc.vector.tensor_copy(out=rb[:].rearrange("p (e h) -> p e h", h=UH), in_=rb0[:].rearrange("p (h e) -> p e h", h=UH))
+
+        def bias_tables(bps):
+            nc.vector.tensor_copy(out=bt[:].rearrange("p t u -> p (t u)"), in_=bps)
+            for j in range(2):
+                for s_ in range(2):
                     nc.vector.tensor_tensor(
-                        out=zr[:, s_, c, :].rearrange("p (z r) -> p z r", z=2),
-                        in0=tz[:, 0:2].unsqueeze(2).to_broadcast([P, 2, 8]),
-                        in1=tr.unsqueeze(1).to_broadcast([P, 2, 8]), op=op,
-                    )
-                    nc.vector.tensor_tensor(
-                        out=tab[:, s_, c, :].rearrange("p (a zr wh) -> p zr wh a", a=4, zr=16),
-                        in0=zr[:, s_, c, :].unsqueeze(2).unsqueeze(3).to_broadcast([P, 16, 2, 4]),
-                        in1=tw.rearrange("p (wh a) -> p wh a", wh=2).unsqueeze(1).to_broadcast([P, 16, 2, 4]), op=op,
-                    )
-            for c in range(RT):
-                for s_, full in ((0, cos_t[c]), (1, sin_t[c])):
-                    nc.vector.tensor_copy(
-                        out=full[:].rearrange("p (n w) -> p n w", w=NWIN),
-                        in_=tab[:, s_, c, :].unsqueeze(2).to_broadcast([P, 128, NWIN]),
+                        out=bcs[:, s_, :, 4 * j : 4 * j + 4, :],
+                        in0=cs[:, j, s_, :].unsqueeze(1).unsqueeze(2).to_broadcast([P, 3, 4, 8]),
+                        in1=bt[:, :, 4 * j : 4 * j + 4].unsqueeze(3).to_broadcast([P, 3, 4, 8]), op=ALU.mult,
                     )
 
-        bt = const.tile([P, 24], F32, name="bt")
+        tsin = {}
+        for third in range(3):
+            for half in range(2):
+                ts_ = const.tile([P, 512], F32, name="tsin%d_%d" % (third, half))
+                nc.gpsimd.memset(pos_view(ts_[:], third, 0), 0.0)
+                tsin[(third, half)] = ts_
 
         xcodes = const.tile([P, PASSES, 512], U32, name="xcodes", align_bytes=64)
         xplanes = const.tile([P, PASSES, 512], U8, name="xplanes", align_bytes=64)
@@ -179,11 +173,11 @@ def tile_windowattention_pa_kernel(tc, x, qkv_w_bytes, qkv_w_scale, qkv_b, out_0
         st_prod = {}
         st_out = {}
 
-        def cast(i):
-            wb = work.tile([P, RT, K], BF16, name="wb", tag="wb", bufs=3)
-            for r in range(RT):
-                nc.scalar.copy(out=wb[:, r, :], in_=st_bytes[i][:, r, :].bitcast(FP8))
-            st_wb[i] = wb
+        def cast(i, r):
+            if r == 0:
+                wb = work.tile([P, RT, K], BF16, name="wb", tag="wb", bufs=3)
+                st_wb[i] = wb
+            nc.scalar.copy(out=st_wb[i][:, r, :], in_=st_bytes[i][:, r, :].bitcast(FP8))
 
         def t_pair(i, g):
             wt = ps_tp.tile([P, 2, 2 * P], F32, name="wt2", tag="tp")
@@ -191,9 +185,9 @@ def tile_windowattention_pa_kernel(tc, x, qkv_w_bytes, qkv_w_scale, qkv_b, out_0
                 words = st_wb[i][:, r, :].bitcast(F32)
                 for u in range(2):
                     nc.tensor.transpose(
-                        wt[:, u, r * P : (r + 1) * P], words[:, 256 * g + u : 256 * (g + 1) : 2], ident_f[:]
+                        wt[:, u, r * P : (r + 1) * P], words[:, 256 * g + u : 256 * (g + 1) : 2], sort_p[:]
                     )
-            return [(wt[:], g, 0, 2 * P)]
+            return [(wt[:], g, 0, 2)]
 
         def t_third(i, gs):
             wt = ps_tp.tile([P, 2, 2, P], F32, name="wt3", tag="tp")
@@ -201,16 +195,18 @@ def tile_windowattention_pa_kernel(tc, x, qkv_w_bytes, qkv_w_scale, qkv_b, out_0
             jobs = []
             for gi, g in enumerate(gs):
                 for u in range(2):
-                    nc.tensor.transpose(wt[:, gi, u, :], words[:, 256 * g + u : 256 * (g + 1) : 2], ident_f[:])
-                jobs.append((wt[:, gi], g, 2 * P, P))
+                    nc.tensor.transpose(wt[:, gi, u, :], words[:, 256 * g + u : 256 * (g + 1) : 2], sort_p[:])
+                jobs.append((wt[:, gi], g, 2, 1))
             return jobs
 
         def scaled_out(i, job):
-            src, g, col0, cols = job
+            src, g, r0, nr = job
+            n16 = 16 * nr
+            dst = st_g[i][:, g, :].rearrange("p (c r x) -> p r c x", r=RT, x=32)[:, r0 : r0 + nr]
             nc.vector.tensor_tensor(
-                out=st_g[i][:, g, 4 * col0 : 4 * (col0 + cols)].rearrange("p (c u e) -> p c u e", u=2, e=2),
-                in0=src.rearrange("p u c -> p (u c)").bitcast(BF16).rearrange("p (u c e) -> p c u e", u=2, e=2),
-                in1=scale[:, g, :].rearrange("p (u e) -> p u e", e=2).unsqueeze(1).to_broadcast([P, cols, 2, 2]),
+                out=dst,
+                in0=src.rearrange("p u c -> p (u c)").bitcast(BF16).rearrange("p (u rc h e) -> p rc h u e", u=2, h=UH, e=2),
+                in1=scale[:, g, :].rearrange("p (u e) -> p u e", e=2).unsqueeze(1).to_broadcast([P, n16 * UH, 2, 2]),
                 op=ALU.mult,
             )
 
@@ -239,21 +235,18 @@ def tile_windowattention_pa_kernel(tc, x, qkv_w_bytes, qkv_w_scale, qkv_b, out_0
                 )
             return mm
 
-        def biased(i, c, mm):
-            j = ORDER[i][0]
-            y = work.tile([P, 512], F32, name="y", tag="y", bufs=4)
-            col = first_tile(i) + c
-            nc.scalar.activation(
-                out=y[:], in_=mm[:], func=ACT.Identity, scale=SCALE if j == 0 else 1.0, bias=bt[:, col : col + 1]
-            )
-            return y
-
-        def products(i, c, y):
-            ya = work.tile([P, 512], F32, name="ya", tag="ya", bufs=6)
-            nc.gpsimd.tensor_tensor(out=ya[:], in0=y[:], in1=cos_t[c][:], op=ALU.mult)
-            yb = work.tile([P, 512], F32, name="yb", tag="yb", bufs=6)
-            nc.gpsimd.tensor_tensor(out=yb[:], in0=y[:], in1=sin_t[c][:], op=ALU.mult)
-            st_prod[(i, c)] = (ya, yb)
+        def products(i, c, mm):
+            j, un = ORDER[i]
+            npos = 2 if c == 0 else 8
+            o_ = work.tile([P, 512], F32, name="o", tag="o", bufs=6)
+            t_ = tsin[(c, i % 2)]
+            for s_, dst in ((0, o_), (1, t_)):
+                for pos in range(s_, npos):
+                    nc.scalar.activation(
+                        out=pos_view(dst[:], c, pos), in_=pos_view(mm[:], c, pos), func=ACT.Identity,
+                        scale=cs[:, j, s_, pos : pos + 1], bias=bcs[:, s_, c, 4 * j + un, pos : pos + 1],
+                    )
+            st_prod[(i, c)] = (o_, t_)
 
         def back_t(i, a):
             tb = ps_tb.tile([P, UCOLS], F32, name="tb", tag="tb")
@@ -262,7 +255,7 @@ def tile_windowattention_pa_kernel(tc, x, qkv_w_bytes, qkv_w_scale, qkv_b, out_0
                 ya, yb = st_prod[(i, c)]
                 dst = tb[:, c * P : (c + 1) * P]
                 nc.tensor.matmul(out=dst, lhsT=ya[:, toks], rhs=ident_f[:], is_transpose=True, start=True, stop=False)
-                nc.tensor.matmul(out=dst, lhsT=yb[:, toks], rhs=perm[:], is_transpose=True, start=False, stop=True)
+                nc.tensor.matmul(out=dst, lhsT=yb[:, toks], rhs=swap_p[:], is_transpose=True, start=False, stop=True)
             return tb
 
         def store(i, stg):
@@ -277,7 +270,7 @@ def tile_windowattention_pa_kernel(tc, x, qkv_w_bytes, qkv_w_scale, qkv_b, out_0
             if a == 0:
                 stg_new = work.tile([P, UH, 4, HD], F32, name="stg", tag="stg", bufs=3)
                 st_out[i] = stg_new
-            nc.scalar.copy(out=st_out[i][:, :, a, :], in_=tb[:].rearrange("p (h e) -> p h e", e=HD))
+            nc.scalar.copy(out=st_out[i][:, :, a, :], in_=tb[:].rearrange("p (e h) -> p h e", h=UH))
             if a == 3:
                 store(i, st_out[i])
 
@@ -301,59 +294,66 @@ def tile_windowattention_pa_kernel(tc, x, qkv_w_bytes, qkv_w_scale, qkv_b, out_0
                 sv_new = work.tile([P, UH, 4, HD], F32, name="sv", tag="sv", bufs=3)
                 st_out[i] = sv_new
             nc.vector.tensor_tensor(
-                out=st_out[i][:, :, a, :], in0=mm[:, 0:UCOLS].rearrange("p (h e) -> p h e", e=HD),
+                out=st_out[i][:, :, a, :], in0=mm[:, 0:UCOLS].rearrange("p (e h) -> p h e", h=UH),
                 in1=bias_v[:, UH * un : UH * (un + 1), :], op=ALU.add,
             )
             if a == 3:
                 store(i, st_out[i])
 
-        cast(0)
+        cast(0, 0)
         nc.scalar.activation(out=trig[:], in_=wrap[:], func=ACT.Sin)
+        cast(0, 1)
+        cast(0, 2)
         for s in range(n_units + 3):
             if 1 <= s and s + 2 < n_units:
                 load(s + 2)
-            if s + 1 < n_units:
-                cast(s + 1)
-            jobs = []
-            if s < n_units:
+            now = s < n_units
+            prev = 1 <= s <= n_units
+            prev_v = prev and ORDER[s - 1][0] == 2
+            back = 2 <= s <= n_units + 1 and ORDER[s - 2][0] != 2
+            if now:
                 grp = work.tile([P, PASSES, 4 * UCOLS], BF16, name="grp", tag="grp", bufs=2, align_bytes=64)
                 st_g[s] = grp
-                for g in range(PASSES):
-                    jobs.extend(t_pair(s, g))
-                jobs.extend(t_third(s, (0, 1)))
-            prev_v = 1 <= s <= n_units and ORDER[s - 1][0] == 2
-            if 1 <= s <= n_units:
+
+            for ph in range(3):
+                if s + 1 < n_units and s > 0:
+                    cast(s + 1, ph)
+                jobs = []
+                if now:
+                    if ph == 0:
+                        jobs = t_pair(s, 0) + t_pair(s, 1)
+                    elif ph == 1:
+                        jobs = t_pair(s, 2) + t_third(s, (0, 1))
+                    else:
+                        jobs = t_third(s, (2,))
                 if prev_v:
-                    for a in range(4):
+                    for a in ((0,), (1, 2), (3,))[ph]:
                         mm = v_bank(s - 1, a)
-                        if a < len(jobs):
-                            scaled_out(s, jobs[a])
+                        if jobs:
+                            scaled_out(s, jobs.pop(0))
                         v_out(s - 1, a, mm)
-                    jobs = jobs[4:]
-                else:
-                    for c in range(RT):
-                        mm = mx_tile(s - 1, c)
-                        y = biased(s - 1, c, mm)
-                        products(s - 1, c, y)
-            for job in jobs:
-                scaled_out(s, job)
-            if s < n_units:
-                for job in t_third(s, (2,)):
+                elif prev:
+                    products(s - 1, ph, mx_tile(s - 1, ph))
+                for job in jobs:
                     scaled_out(s, job)
-                quant(s)
+                if back:
+                    for a in ((0,), (1, 2), (3,))[ph]:
+                        back_out(s - 2, a, back_t(s - 2, a))
             if s == 0:
                 for g in range(PASSES):
                     x_pass(g)
-                bps = ps_tb.tile([P, UCOLS], F32, name="bps", tag="tb")
-                nc.tensor.matmul(out=bps[:, 0:24], lhsT=rb0[:], rhs=ident_b[:, 0:24], start=True, stop=True)
+                for r in range(RT):
+                    cast(1, r)
+            if now:
+                quant(s)
+            if s == 0:
                 for g in range(PASSES):
                     x_quant(g)
-                nc.vector.tensor_scalar(out=bt[:, 0:12], in0=bps[:, 0:12], scalar1=SCALE, scalar2=None, op0=ALU.mult)
-                nc.vector.tensor_copy(out=bt[:, 12:24], in_=bps[:, 12:24])
+                bps = ps_tb.tile([P, UCOLS], F32, name="bps", tag="tb")
                 trig_tables()
+                nc.tensor.matmul(out=bps[:, 0:24], lhsT=rb[:], rhs=ident_b[:, 0:24], start=True, stop=True)
+                bias_tables(bps[:, 0:24])
+            if s == 1:
                 nc.sync.dma_start(
                     out=bias_v[:].rearrange("p h e -> p (h e)"), in_=qkv_b[2 * JROWS :].partition_broadcast(P)
                 )
-            if 2 <= s <= n_units + 1 and ORDER[s - 2][0] != 2:
-                for a in range(4):
-                    back_out(s - 2, a, back_t(s - 2, a))

@@ -31,6 +31,19 @@ FLOPS = 2 * 512 * 4608 * 1536
 ORDER = ((0, 0), (0, 1), (2, 0), (0, 2), (0, 3), (2, 1), (1, 0), (1, 1), (2, 2), (1, 2), (1, 3), (2, 3))
 
 
+BV = ()
+PLAN = (
+    (((0, 2, (0,)), (0, 2, (1,))), ((0, 2, (2,)), (2, 1, (0, 1))), ((2, 1, (2,)),)),
+    (((2, 1, (0, 1)), (2, 1, (2,)), (0, 2, (0,))), ((0, 2, (1,)),), ((0, 2, (2,)),)),
+    (((1, 2, (0,)), (0, 1, (0, 1))), ((1, 2, (1,)), (0, 1, (2,))), ((1, 2, (2,)),)),
+)
+GCH = 512
+VS = ()
+AHEAD = 1
+LAG = 1
+GS = (0,) * 12
+
+
 def pos_view(ap, third, pos):
     if third == 0:
         return ap.rearrange("p (a z y) -> p a z y", a=4, z=2)[:, :, pos, :]
@@ -57,7 +70,7 @@ def tile_windowattention_pa_kernel(tc, x, qkv_w_bytes, qkv_w_scale, qkv_b, out_0
         def load(i):
             j, un = ORDER[i]
             rows = qkv_w_bytes[JROWS * j + UCOLS * un : JROWS * j + UCOLS * (un + 1), :].rearrange("(p r) k -> p r k", r=RT)
-            b_ = work.tile([P, RT, K], U8, name="wbytes", tag="wbytes", bufs=4)
+            b_ = work.tile([P, RT, K], U8, name="wbytes", tag="wbytes", bufs=5)
             nc.sync.dma_start(out=b_[:, 0, :], in_=rows[:, 0, :])
             nc.sync.dma_start(out=b_[:, 1:RT, :], in_=rows[:, 1:RT, :])
             st_bytes[i] = b_
@@ -67,21 +80,29 @@ def tile_windowattention_pa_kernel(tc, x, qkv_w_bytes, qkv_w_scale, qkv_b, out_0
         ident_b = const.tile([P, P], BF16, name="ident_b")
         make_identity(nc, ident_b[:])
 
+        load(0)
         rb0 = const.tile([P, P], BF16, name="rb0")
         nc.vector.memset(rb0[:], 0.0)
         for t in range(3):
-            nc.gpsimd.dma_start(
-                out=rb0[8 * t : 8 * t + 8, :].rearrange("u (h e) -> u h e", e=16),
-                in_=qkv_b[0 : 2 * JROWS].rearrange("(u h t e) -> t u h e", u=8, h=UH, e=16)[t],
+            nc.sync.dma_start(
+                out=rb0[12 * t : 12 * t + 12, :].rearrange("u (h e) -> u h e", e=16),
+                in_=qkv_b.rearrange("(u h t e) -> t u h e", u=12, h=UH, e=16)[t],
             )
-        load(0)
         scale = const.tile([P, PASSES, 4], F32, name="scale")
         nc.sync.dma_start(out=scale[:], in_=qkv_w_scale.rearrange("o (g p t) -> p (o g) t", p=P, t=4))
+        sbc = const.tile([P, K], F32, name="sbc")
         x_all = const.tile([P, NWIN, K], BF16, name="x_all")
         for w in range(2):
             nc.sync.dma_start(out=x_all[:, 2 * w : 2 * w + 2, :], in_=x[2 * w : 2 * w + 2].rearrange("w p k -> p w k"))
         load(1)
+        for g in range(PASSES if any(GS) else 0):
+            nc.sync.dma_start(
+                out=sbc[:, 512 * g : 512 * (g + 1)],
+                in_=qkv_w_scale.rearrange("o k -> (o k)")[512 * g : 512 * (g + 1)].partition_broadcast(P),
+            )
         load(2)
+        if AHEAD == 2:
+            load(3)
         bias_v = const.tile([P, HEADS, HD], BF16, name="bias_v")
 
         warm = const.tile([P, 1], F32, name="warm")
@@ -120,7 +141,7 @@ def tile_windowattention_pa_kernel(tc, x, qkv_w_bytes, qkv_w_scale, qkv_b, out_0
         nc.vector.tensor_tensor(out=wrap[:], in0=wrap[:], in1=angle[:], op=ALU.add)
         trig = const.tile([P, 2, 8], F32, name="trig")
         cs = const.tile([P, 2, 2, 8], F32, name="cs")
-        bt = const.tile([P, 3, 8], F32, name="bt")
+        bt = const.tile([P, 3, 12], F32, name="bt")
         bcs = const.tile([P, 2, 3, 8, 8], F32, name="bcs")
         rb = const.tile([P, P], BF16, name="rb")
 
@@ -129,9 +150,12 @@ def tile_windowattention_pa_kernel(tc, x, qkv_w_bytes, qkv_w_scale, qkv_b, out_0
                 sc = SCALE if j == 0 else 1.0
                 nc.vector.tensor_scalar(out=cs[:, j, 0, :], in0=trig[:, 0, :], scalar1=sc, scalar2=None, op0=ALU.mult)
                 nc.vector.tensor_scalar(out=cs[:, j, 1, :], in0=trig[:, 1, :], scalar1=sgn[:], scalar2=sc, op0=ALU.mult, op1=ALU.mult)
-            nc.vector.tensor_copy(out=rb[:].rearrange("p (e h) -> p e h", h=UH), in_=rb0[:].rearrange("p (h e) -> p e h", h=UH))
 
-        def bias_tables(bps):
+        def bias_tables():
+            nc.vector.tensor_copy(out=rb[:].rearrange("p (e h) -> p e h", h=UH), in_=rb0[:].rearrange("p (h e) -> p e h", h=UH))
+            bps_t = ps_tb.tile([P, UCOLS], F32, name="bps", tag="tb")
+            nc.tensor.matmul(out=bps_t[:, 0:36], lhsT=rb[:], rhs=ident_b[:, 0:36], start=True, stop=True)
+            bps = bps_t[:, 0:36]
             nc.vector.tensor_copy(out=bt[:].rearrange("p t u -> p (t u)"), in_=bps)
             for j in range(2):
                 for s_ in range(2):
@@ -155,7 +179,10 @@ def tile_windowattention_pa_kernel(tc, x, qkv_w_bytes, qkv_w_scale, qkv_b, out_0
         def x_pass(g):
             gxw = gx_all[:, g, :].bitcast(F32).rearrange("p (a m wp y) -> p wp a m y", a=4, m=32, wp=2)
             for wp in range(2):
-                wt = ps_tp.tile([P, 4, P], F32, name="wt", tag="tp")
+                if wp == 0:
+                    wt = ps_mm.tile([P, 4, P], F32, name="wt", tag="mm")
+                else:
+                    wt = ps_tb.tile([P, 4, P], F32, name="wt", tag="tb")
                 for win2 in range(2):
                     words = x_all[:, 2 * wp + win2, :].bitcast(F32)
                     for u in range(2):
@@ -168,41 +195,65 @@ def tile_windowattention_pa_kernel(tc, x, qkv_w_bytes, qkv_w_scale, qkv_b, out_0
             nc.vector.quantize_mx(out=xcodes[:, g, :].bitcast(FP8X4), scales=xplanes[:, g, :], in_=gx_all[:, g, :])
 
         st_wb = {}
+        st_ws = {}
         st_g = {}
         st_codes = {}
         st_prod = {}
         st_out = {}
 
         def cast(i, r):
-            if r == 0:
-                wb = work.tile([P, RT, K], BF16, name="wb", tag="wb", bufs=3)
+            if i not in st_wb:
+                wb = work.tile([P, RT, K], BF16, name="wb", tag="wb", bufs=AHEAD + 2)
                 st_wb[i] = wb
             nc.scalar.copy(out=st_wb[i][:, r, :], in_=st_bytes[i][:, r, :].bitcast(FP8))
-
-        def t_pair(i, g):
-            wt = ps_tp.tile([P, 2, 2 * P], F32, name="wt2", tag="tp")
-            for r in range(2):
-                words = st_wb[i][:, r, :].bitcast(F32)
-                for u in range(2):
-                    nc.tensor.transpose(
-                        wt[:, u, r * P : (r + 1) * P], words[:, 256 * g + u : 256 * (g + 1) : 2], sort_p[:]
+            if r >= RT - GS[i]:
+                ws = work.tile([P, K], BF16, name="ws", tag="ws", bufs=3)
+                for k0 in range(0, K, GCH):
+                    ks = slice(k0, k0 + GCH)
+                    nc.gpsimd.tensor_tensor(
+                        out=ws[:, 512 * (k0 // 512) : 512 * (k0 // 512) + 512].rearrange("p (u m e) -> p u m e", u=2, e=2)[:, :, (k0 % 512) // 4 : (k0 % 512 + GCH) // 4, :],
+                        in0=st_wb[i][:, r, ks].rearrange("p (m u e) -> p u m e", u=2, e=2),
+                        in1=sbc[:, ks].rearrange("p (m u e) -> p u m e", u=2, e=2), op=ALU.mult,
                     )
-            return [(wt[:], g, 0, 2)]
+                st_ws[(i, r)] = ws
 
-        def t_third(i, gs):
-            wt = ps_tp.tile([P, 2, 2, P], F32, name="wt3", tag="tp")
-            words = st_wb[i][:, 2, :].bitcast(F32)
+        def words_of(i, r, g, u):
+            if r >= RT - GS[i]:
+                return st_ws[(i, r)][:].bitcast(F32)[:, 256 * g + P * u : 256 * g + P * (u + 1)]
+            return st_wb[i][:, r, :].bitcast(F32)[:, 256 * g + u : 256 * (g + 1) : 2]
+
+        def rows_view(i, g, r0, nr):
+            return st_g[i][:, g, :].rearrange("p (c r x) -> p r c x", r=RT, x=32)[:, r0 : r0 + nr]
+
+        def t_bank(i, spec):
+            r0, nr, gs = spec
             jobs = []
-            for gi, g in enumerate(gs):
-                for u in range(2):
-                    nc.tensor.transpose(wt[:, gi, u, :], words[:, 256 * g + u : 256 * (g + 1) : 2], sort_p[:])
-                jobs.append((wt[:, gi], g, 2, 1))
+            if nr == 2:
+                wt = ps_tp.tile([P, 2, 2 * P], F32, name="wt2", tag="tp")
+                for r in range(2):
+                    for u in range(2):
+                        nc.tensor.transpose(wt[:, u, r * P : (r + 1) * P], words_of(i, r0 + r, gs[0], u), sort_p[:])
+                parts = [wt[:]]
+            else:
+                wt3 = ps_tp.tile([P, 2, 2, P], F32, name="wt3", tag="tp")
+                for gi, g in enumerate(gs):
+                    for u in range(2):
+                        nc.tensor.transpose(wt3[:, gi, u, :], words_of(i, r0, g, u), sort_p[:])
+                parts = [wt3[:, gi] for gi in range(len(gs))]
+            for src, g in zip(parts, gs):
+                if r0 >= RT - GS[i]:
+                    nc.scalar.copy(
+                        out=rows_view(i, g, r0, nr).bitcast(F32),
+                        in_=src.rearrange("p u (r c h) -> p r c h u", r=nr, h=UH),
+                    )
+                else:
+                    jobs.append((src, g, r0, nr))
             return jobs
 
         def scaled_out(i, job):
             src, g, r0, nr = job
             n16 = 16 * nr
-            dst = st_g[i][:, g, :].rearrange("p (c r x) -> p r c x", r=RT, x=32)[:, r0 : r0 + nr]
+            dst = rows_view(i, g, r0, nr)
             nc.vector.tensor_tensor(
                 out=dst,
                 in0=src.rearrange("p u c -> p (u c)").bitcast(BF16).rearrange("p (u rc h e) -> p rc h u e", u=2, h=UH, e=2),
@@ -211,8 +262,8 @@ def tile_windowattention_pa_kernel(tc, x, qkv_w_bytes, qkv_w_scale, qkv_b, out_0
             )
 
         def quant(i):
-            codes = work.tile([P, PASSES, UCOLS], U32, name="codes", tag="codes", bufs=2, align_bytes=64)
-            planes = work.tile([P, PASSES, UCOLS], U8, name="planes", tag="planes", bufs=2, align_bytes=64)
+            codes = work.tile([P, PASSES, UCOLS], U32, name="codes", tag="codes", bufs=3, align_bytes=64)
+            planes = work.tile([P, PASSES, UCOLS], U8, name="planes", tag="planes", bufs=3, align_bytes=64)
             cf = codes[:].rearrange("p g c -> p (g c)")
             pf = planes[:].rearrange("p g c -> p (g c)")
             gf = st_g[i][:].rearrange("p g c -> p (g c)")
@@ -238,7 +289,12 @@ def tile_windowattention_pa_kernel(tc, x, qkv_w_bytes, qkv_w_scale, qkv_b, out_0
         def products(i, c, mm):
             j, un = ORDER[i]
             npos = 2 if c == 0 else 8
-            o_ = work.tile([P, 512], F32, name="o", tag="o", bufs=6)
+            if j == 2:
+                o_ = work.tile([P, 512], F32, name="o", tag="o", bufs=8)
+                nc.scalar.activation(out=o_[:], in_=mm[:], func=ACT.Identity, bias=bt[:, c, 8 + un : 9 + un])
+                st_prod[(i, c)] = (o_, None)
+                return
+            o_ = work.tile([P, 512], F32, name="o", tag="o", bufs=8)
             t_ = tsin[(c, i % 2)]
             for s_, dst in ((0, o_), (1, t_)):
                 for pos in range(s_, npos):
@@ -254,6 +310,9 @@ def tile_windowattention_pa_kernel(tc, x, qkv_w_bytes, qkv_w_scale, qkv_b, out_0
             for c in range(RT):
                 ya, yb = st_prod[(i, c)]
                 dst = tb[:, c * P : (c + 1) * P]
+                if yb is None:
+                    nc.tensor.transpose(dst, ya[:, toks], ident_f[:])
+                    continue
                 nc.tensor.matmul(out=dst, lhsT=ya[:, toks], rhs=ident_f[:], is_transpose=True, start=True, stop=False)
                 nc.tensor.matmul(out=dst, lhsT=yb[:, toks], rhs=swap_p[:], is_transpose=True, start=False, stop=True)
             return tb
@@ -270,7 +329,10 @@ def tile_windowattention_pa_kernel(tc, x, qkv_w_bytes, qkv_w_scale, qkv_b, out_0
             if a == 0:
                 stg_new = work.tile([P, UH, 4, HD], F32, name="stg", tag="stg", bufs=3)
                 st_out[i] = stg_new
-            nc.scalar.copy(out=st_out[i][:, :, a, :], in_=tb[:].rearrange("p (e h) -> p h e", h=UH))
+            if a in BV:
+                nc.vector.tensor_copy(out=st_out[i][:, :, a, :], in_=tb[:].rearrange("p (e h) -> p h e", h=UH))
+            else:
+                nc.scalar.copy(out=st_out[i][:, :, a, :], in_=tb[:].rearrange("p (e h) -> p h e", h=UH))
             if a == 3:
                 store(i, st_out[i])
 
@@ -289,13 +351,12 @@ def tile_windowattention_pa_kernel(tc, x, qkv_w_bytes, qkv_w_scale, qkv_b, out_0
             return mm
 
         def v_out(i, a, mm):
-            un = ORDER[i][1]
             if a == 0:
                 sv_new = work.tile([P, UH, 4, HD], F32, name="sv", tag="sv", bufs=3)
                 st_out[i] = sv_new
             nc.vector.tensor_tensor(
                 out=st_out[i][:, :, a, :], in0=mm[:, 0:UCOLS].rearrange("p (e h) -> p h e", h=UH),
-                in1=bias_v[:, UH * un : UH * (un + 1), :], op=ALU.add,
+                in1=bias_v[:, UH * ORDER[i][1] : UH * (ORDER[i][1] + 1), :], op=ALU.add,
             )
             if a == 3:
                 store(i, st_out[i])
@@ -304,55 +365,49 @@ def tile_windowattention_pa_kernel(tc, x, qkv_w_bytes, qkv_w_scale, qkv_b, out_0
         nc.scalar.activation(out=trig[:], in_=wrap[:], func=ACT.Sin)
         cast(0, 1)
         cast(0, 2)
+        trig_tables()
+        bias_tables()
         for s in range(n_units + 3):
-            if 1 <= s and s + 2 < n_units:
-                load(s + 2)
-            now = s < n_units
-            prev = 1 <= s <= n_units
-            prev_v = prev and ORDER[s - 1][0] == 2
-            back = 2 <= s <= n_units + 1 and ORDER[s - 2][0] != 2
-            if now:
+            if 1 <= s and s + 1 + AHEAD < n_units:
+                load(s + 1 + AHEAD)
+            if s < n_units:
                 grp = work.tile([P, PASSES, 4 * UCOLS], BF16, name="grp", tag="grp", bufs=2, align_bytes=64)
                 st_g[s] = grp
-
             for ph in range(3):
-                if s + 1 < n_units and s > 0:
-                    cast(s + 1, ph)
+                ca = s + AHEAD
+                if s > 0 and ca < n_units:
+                    cast(ca, (2, 0, 1)[ph])
                 jobs = []
-                if now:
-                    if ph == 0:
-                        jobs = t_pair(s, 0) + t_pair(s, 1)
-                    elif ph == 1:
-                        jobs = t_pair(s, 2) + t_third(s, (0, 1))
+                if s < n_units:
+                    for spec in PLAN[GS[s]][ph]:
+                        jobs.extend(t_bank(s, spec))
+                s1, ph1 = divmod(3 * s + ph - 3 - LAG, 3)
+                s2, ph2 = divmod(3 * s + ph - 6 - LAG, 3)
+                if 0 <= s1 < n_units:
+                    if ORDER[s1][0] == 2 and s1 not in VS:
+                        for a in ((0,), (1, 2), (3,))[ph1]:
+                            mm = v_bank(s1, a)
+                            if jobs:
+                                scaled_out(s, jobs.pop(0))
+                            v_out(s1, a, mm)
                     else:
-                        jobs = t_third(s, (2,))
-                if prev_v:
-                    for a in ((0,), (1, 2), (3,))[ph]:
-                        mm = v_bank(s - 1, a)
-                        if jobs:
-                            scaled_out(s, jobs.pop(0))
-                        v_out(s - 1, a, mm)
-                elif prev:
-                    products(s - 1, ph, mx_tile(s - 1, ph))
+                        products(s1, ph1, mx_tile(s1, ph1))
                 for job in jobs:
                     scaled_out(s, job)
-                if back:
-                    for a in ((0,), (1, 2), (3,))[ph]:
-                        back_out(s - 2, a, back_t(s - 2, a))
+                if 0 <= s2 < n_units and (ORDER[s2][0] != 2 or s2 in VS):
+                    for a in ((0,), (1, 2), (3,))[ph2]:
+                        back_out(s2, a, back_t(s2, a))
             if s == 0:
                 for g in range(PASSES):
                     x_pass(g)
-                for r in range(RT):
-                    cast(1, r)
-            if now:
+                for i in range(1, AHEAD + 1):
+                    for r in (2, 0, 1):
+                        cast(i, r)
+            if s < n_units:
                 quant(s)
             if s == 0:
                 for g in range(PASSES):
                     x_quant(g)
-                bps = ps_tb.tile([P, UCOLS], F32, name="bps", tag="tb")
-                trig_tables()
-                nc.tensor.matmul(out=bps[:, 0:24], lhsT=rb[:], rhs=ident_b[:, 0:24], start=True, stop=True)
-                bias_tables(bps[:, 0:24])
             if s == 1:
                 nc.sync.dma_start(
                     out=bias_v[:].rearrange("p h e -> p (h e)"), in_=qkv_b[2 * JROWS :].partition_broadcast(P)

import math
from contextlib import ExitStack

import concourse.mybir as mybir
from concourse.masks import make_identity

F32 = mybir.dt.float32
BF16 = mybir.dt.bfloat16
U32 = mybir.dt.uint32
U8 = mybir.dt.uint8
FP8 = mybir.dt.float8_e4m3fn
FP8X4 = mybir.dt.float8_e4m3fn_x4
ALU = mybir.AluOpType
ACT = mybir.ActivationFunctionType
AX = mybir.AxisListType

P = 128
K = 1536
PASSES = 3
NWIN = 4
HEADS = 32
HD = 48
RT = 3
UH = 8
UCOLS = RT * P
JROWS = HEADS * HD
SCALE = HD ** -0.5
OMEGA = [10000.0 ** (-i / 8.0) for i in range(8)]

FLOPS = 2 * 512 * 4608 * 1536
ORDER = ((0, 0), (0, 1), (2, 0), (0, 2), (0, 3), (2, 1), (1, 0), (1, 1), (2, 2), (1, 2), (1, 3), (2, 3))


BV = ()
PLAN = (
    (((0, 2, (0,)), (0, 2, (1,))), ((0, 2, (2,)), (2, 1, (0, 1))), ((2, 1, (2,)),)),
    (((2, 1, (0, 1)), (2, 1, (2,)), (0, 2, (0,))), ((0, 2, (1,)),), ((0, 2, (2,)),)),
    (((1, 2, (0,)), (0, 1, (0, 1))), ((1, 2, (1,)), (0, 1, (2,))), ((1, 2, (2,)),)),
)
GCH = 512
VS = ()
AHEAD = 1
LAG = 1
GS = (0,) * 12


def pos_view(ap, third, pos):
    if third == 0:
        return ap.rearrange("p (a z y) -> p a z y", a=4, z=2)[:, :, pos, :]
    if third == 1:
        return ap.rearrange("p (az r y) -> p az r y", az=8, r=8)[:, :, pos, :]
    return ap.rearrange("p (a zr wh win) -> p a zr wh win", a=4, zr=16, wh=2)[:, pos % 4, :, pos // 4, :]


def tile_windowattention_pa_kernel(tc, x, qkv_w_bytes, qkv_w_scale, qkv_b, out_0, out_1, out_2):
    nc = tc.nc
    outs = [out_0, out_1, out_2]
    n_units = len(ORDER)

    with ExitStack() as ctx:
        const = ctx.enter_context(tc.tile_pool(name="const", bufs=1))
        work = ctx.enter_context(tc.tile_pool(name="work", bufs=2))
        ps_tp = ctx.enter_context(tc.psum_pool(name="ps_tp", bufs=4))
        ps_mm = ctx.enter_context(tc.psum_pool(name="ps_mm", bufs=2))
        ps_tb = ctx.enter_context(tc.psum_pool(name="ps_tb", bufs=2))
        ctx.enter_context(tc.manual_schedule())

        st_bytes = {}

        def load(i):
            j, un = ORDER[i]
            rows = qkv_w_bytes[JROWS * j + UCOLS * un : JROWS * j + UCOLS * (un + 1), :].rearrange("(p r) k -> p r k", r=RT)
            b_ = work.tile([P, RT, K], U8, name="wbytes", tag="wbytes", bufs=5)
            nc.sync.dma_start(out=b_[:, 0, :], in_=rows[:, 0, :])
            nc.sync.dma_start(out=b_[:, 1:RT, :], in_=rows[:, 1:RT, :])
            st_bytes[i] = b_

        ident_f = const.tile([P, P], F32, name="ident_f")
        make_identity(nc, ident_f[:])
        ident_b = const.tile([P, P], BF16, name="ident_b")
        make_identity(nc, ident_b[:])

        load(0)
        rb0 = const.tile([P, P], BF16, name="rb0")
        nc.vector.memset(rb0[:], 0.0)
        for t in range(3):
            nc.sync.dma_start(
                out=rb0[12 * t : 12 * t + 12, :].rearrange("u (h e) -> u h e", e=16),
                in_=qkv_b.rearrange("(u h t e) -> t u h e", u=12, h=UH, e=16)[t],
            )
        scale = const.tile([P, PASSES, 4], F32, name="scale")
        nc.sync.dma_start(out=scale[:], in_=qkv_w_scale.rearrange("o (g p t) -> p (o g) t", p=P, t=4))
        sbc = const.tile([P, K], F32, name="sbc")
        x_all = const.tile([P, NWIN, K], BF16, name="x_all")
        for w in range(2):
            nc.sync.dma_start(out=x_all[:, 2 * w : 2 * w + 2, :], in_=x[2 * w : 2 * w + 2].rearrange("w p k -> p w k"))
        load(1)
        for g in range(PASSES if any(GS) else 0):
            nc.sync.dma_start(
                out=sbc[:, 512 * g : 512 * (g + 1)],
                in_=qkv_w_scale.rearrange("o k -> (o k)")[512 * g : 512 * (g + 1)].partition_broadcast(P),
            )
        load(2)
        if AHEAD == 2:
            load(3)
        bias_v = const.tile([P, HEADS, HD], BF16, name="bias_v")

        warm = const.tile([P, 1], F32, name="warm")
        nc.vector.memset(warm[:], 0.0)
        nc.scalar.activation(out=warm[:], in_=warm[:], func=ACT.Sin)
        posrow = const.tile([P, 8], F32, name="posrow")
        for pos in range(8):
            nc.vector.memset(posrow[:, pos : pos + 1], float(pos))
        sort_p = const.tile([P, P], F32, name="sort_p")
        nc.vector.tensor_copy(
            out=sort_p[:].rearrange("p (c h) -> p c h", h=UH), in_=ident_f[:].rearrange("p (h c) -> p c h", h=UH)
        )
        swap_p = const.tile([P, P], F32, name="swap_p")
        for hf in range(2):
            nc.vector.tensor_copy(out=swap_p[:, 64 * hf : 64 * hf + 64], in_=ident_f[:, 64 - 64 * hf : 128 - 64 * hf])
        oh16 = const.tile([P, 16], F32, name="oh16")
        nc.vector.tensor_reduce(out=oh16[:], in_=ident_f[:].rearrange("p (b y) -> p b y", y=8), axis=AX.X, op=ALU.add)
        oh8 = const.tile([P, 8], F32, name="oh8")
        nc.vector.tensor_tensor(out=oh8[:], in0=oh16[:, 0:8], in1=oh16[:, 8:16], op=ALU.add)
        low = const.tile([P, 1], F32, name="low")
        nc.vector.tensor_reduce(out=low[:], in_=oh16[:, 0:8], axis=AX.X, op=ALU.add)
        om8 = const.tile([P, 8], F32, name="om8")
        for i in range(8):
            nc.vector.tensor_scalar(out=om8[:, i : i + 1], in0=oh8[:, i : i + 1], scalar1=OMEGA[i], scalar2=None, op0=ALU.mult)
        sgn = const.tile([P, 1], F32, name="sgn")
        nc.vector.tensor_scalar(out=sgn[:], in0=low[:], scalar1=2.0, scalar2=-1.0, op0=ALU.mult, op1=ALU.add)
        omega = const.tile([P, 1], F32, name="omega")
        nc.vector.tensor_reduce(out=omega[:], in_=om8[:], axis=AX.X, op=ALU.add)
        angle = const.tile([P, 2, 8], F32, name="angle")
        nc.vector.tensor_scalar(
            out=angle[:, 0, :], in0=posrow[:], scalar1=omega[:], scalar2=math.pi / 2, op0=ALU.mult, op1=ALU.add
        )
        nc.vector.tensor_scalar(out=angle[:, 1, :], in0=posrow[:], scalar1=omega[:], scalar2=None, op0=ALU.mult)
        wrap = const.tile([P, 2, 8], F32, name="wrap")
        nc.vector.tensor_scalar(out=wrap[:], in0=angle[:], scalar1=math.pi, scalar2=-2.0 * math.pi, op0=ALU.is_gt, op1=ALU.mult)
        nc.vector.tensor_tensor(out=wrap[:], in0=wrap[:], in1=angle[:], op=ALU.add)
        trig = const.tile([P, 2, 8], F32, name="trig")
        cs = const.tile([P, 2, 2, 8], F32, name="cs")
        bt = const.tile([P, 3, 12], F32, name="bt")
        bcs = const.tile([P, 2, 3, 8, 8], F32, name="bcs")
        rb = const.tile([P, P], BF16, name="rb")

        def trig_tables():
            for j in range(2):
                sc = SCALE if j == 0 else 1.0
                nc.vector.tensor_scalar(out=cs[:, j, 0, :], in0=trig[:, 0, :], scalar1=sc, scalar2=None, op0=ALU.mult)
                nc.vector.tensor_scalar(out=cs[:, j, 1, :], in0=trig[:, 1, :], scalar1=sgn[:], scalar2=sc, op0=ALU.mult, op1=ALU.mult)

        def bias_tables():
            nc.vector.tensor_copy(out=rb[:].rearrange("p (e h) -> p e h", h=UH), in_=rb0[:].rearrange("p (h e) -> p e h", h=UH))
            bps_t = ps_tb.tile([P, UCOLS], F32, name="bps", tag="tb")
            nc.tensor.matmul(out=bps_t[:, 0:36], lhsT=rb[:], rhs=ident_b[:, 0:36], start=True, stop=True)
            bps = bps_t[:, 0:36]
            nc.vector.tensor_copy(out=bt[:].rearrange("p t u -> p (t u)"), in_=bps)
            for j in range(2):
                for s_ in range(2):
                    nc.vector.tensor_tensor(
                        out=bcs[:, s_, :, 4 * j : 4 * j + 4, :],
                        in0=cs[:, j, s_, :].unsqueeze(1).unsqueeze(2).to_broadcast([P, 3, 4, 8]),
                        in1=bt[:, :, 4 * j : 4 * j + 4].unsqueeze(3).to_broadcast([P, 3, 4, 8]), op=ALU.mult,
                    )

        tsin = {}
        for third in range(3):
            for half in range(2):
                ts_ = const.tile([P, 512], F32, name="tsin%d_%d" % (third, half))
                nc.gpsimd.memset(pos_view(ts_[:], third, 0), 0.0)
                tsin[(third, half)] = ts_

        xcodes = const.tile([P, PASSES, 512], U32, name="xcodes", align_bytes=64)
        xplanes = const.tile([P, PASSES, 512], U8, name="xplanes", align_bytes=64)
        gx_all = const.tile([P, PASSES, 2048], BF16, name="gx_all", align_bytes=64)

        def x_pass(g):
            gxw = gx_all[:, g, :].bitcast(F32).rearrange("p (a m wp y) -> p wp a m y", a=4, m=32, wp=2)
            for wp in range(2):
                if wp == 0:
                    wt = ps_mm.tile([P, 4, P], F32, name="wt", tag="mm")
                else:
                    wt = ps_tb.tile([P, 4, P], F32, name="wt", tag="tb")
                for win2 in range(2):
                    words = x_all[:, 2 * wp + win2, :].bitcast(F32)
                    for u in range(2):
                        nc.tensor.transpose(
                            wt[:, 2 * win2 + u, :], words[:, 256 * g + u : 256 * (g + 1) : 2], ident_f[:]
                        )
                nc.scalar.copy(out=gxw[:, wp], in_=wt[:].rearrange("p y (m a) -> p a m y", a=4))

        def x_quant(g):
            nc.vector.quantize_mx(out=xcodes[:, g, :].bitcast(FP8X4), scales=xplanes[:, g, :], in_=gx_all[:, g, :])

        st_wb = {}
        st_ws = {}
        st_g = {}
        st_codes = {}
        st_prod = {}
        st_out = {}

        def cast(i, r):
            if i not in st_wb:
                wb = work.tile([P, RT, K], BF16, name="wb", tag="wb", bufs=AHEAD + 2)
                st_wb[i] = wb
            nc.scalar.copy(out=st_wb[i][:, r, :], in_=st_bytes[i][:, r, :].bitcast(FP8))
            if r >= RT - GS[i]:
                ws = work.tile([P, K], BF16, name="ws", tag="ws", bufs=3)
                for k0 in range(0, K, GCH):
                    ks = slice(k0, k0 + GCH)
                    nc.gpsimd.tensor_tensor(
                        out=ws[:, 512 * (k0 // 512) : 512 * (k0 // 512) + 512].rearrange("p (u m e) -> p u m e", u=2, e=2)[:, :, (k0 % 512) // 4 : (k0 % 512 + GCH) // 4, :],
                        in0=st_wb[i][:, r, ks].rearrange("p (m u e) -> p u m e", u=2, e=2),
                        in1=sbc[:, ks].rearrange("p (m u e) -> p u m e", u=2, e=2), op=ALU.mult,
                    )
                st_ws[(i, r)] = ws

        def words_of(i, r, g, u):
            if r >= RT - GS[i]:
                return st_ws[(i, r)][:].bitcast(F32)[:, 256 * g + P * u : 256 * g + P * (u + 1)]
            return st_wb[i][:, r, :].bitcast(F32)[:, 256 * g + u : 256 * (g + 1) : 2]

        def rows_view(i, g, r0, nr):
            return st_g[i][:, g, :].rearrange("p (c r x) -> p r c x", r=RT, x=32)[:, r0 : r0 + nr]

        def t_bank(i, spec):
            r0, nr, gs = spec
            jobs = []
            if nr == 2:
                wt = ps_tp.tile([P, 2, 2 * P], F32, name="wt2", tag="tp")
                for r in range(2):
                    for u in range(2):
                        nc.tensor.transpose(wt[:, u, r * P : (r + 1) * P], words_of(i, r0 + r, gs[0], u), sort_p[:])
                parts = [wt[:]]
            else:
                wt3 = ps_tp.tile([P, 2, 2, P], F32, name="wt3", tag="tp")
                for gi, g in enumerate(gs):
                    for u in range(2):
                        nc.tensor.transpose(wt3[:, gi, u, :], words_of(i, r0, g, u), sort_p[:])
                parts = [wt3[:, gi] for gi in range(len(gs))]
            for src, g in zip(parts, gs):
                if r0 >= RT - GS[i]:
                    nc.scalar.copy(
                        out=rows_view(i, g, r0, nr).bitcast(F32),
                        in_=src.rearrange("p u (r c h) -> p r c h u", r=nr, h=UH),
                    )
                else:
                    jobs.append((src, g, r0, nr))
            return jobs

        def scaled_out(i, job):
            src, g, r0, nr = job
            n16 = 16 * nr
            dst = rows_view(i, g, r0, nr)
            nc.vector.tensor_tensor(
                out=dst,
                in0=src.rearrange("p u c -> p (u c)").bitcast(BF16).rearrange("p (u rc h e) -> p rc h u e", u=2, h=UH, e=2),
                in1=scale[:, g, :].rearrange("p (u e) -> p u e", e=2).unsqueeze(1).to_broadcast([P, n16 * UH, 2, 2]),
                op=ALU.mult,
            )

        def quant(i):
            codes = work.tile([P, PASSES, UCOLS], U32, name="codes", tag="codes", bufs=3, align_bytes=64)
            planes = work.tile([P, PASSES, UCOLS], U8, name="planes", tag="planes", bufs=3, align_bytes=64)
            cf = codes[:].rearrange("p g c -> p (g c)")
            pf = planes[:].rearrange("p g c -> p (g c)")
            gf = st_g[i][:].rearrange("p g c -> p (g c)")
            for c0, cn in ((0, 1024), (1024, 128)):
                nc.vector.quantize_mx(
                    out=cf[:, c0 : c0 + cn].bitcast(FP8X4), scales=pf[:, c0 : c0 + cn], in_=gf[:, 4 * c0 : 4 * (c0 + cn)]
                )
            st_codes[i] = (codes, planes)

        def mx_tile(i, c):
            codes, planes = st_codes[i]
            mm = ps_mm.tile([P, 512], F32, name="mm", tag="mm")
            cols = slice(c * P, (c + 1) * P)
            for g in range(PASSES):
                nc.tensor.matmul_mx(
                    out=mm[:],
                    lhsT=codes[:, g, cols].bitcast(FP8X4), lhsT_scale=planes[:, g, cols],
                    rhs=xcodes[:, g, :].bitcast(FP8X4), rhs_scale=xplanes[:, g, :],
                    start=(g == 0), stop=(g == PASSES - 1),
                )
            return mm

        def products(i, c, mm):
            j, un = ORDER[i]
            npos = 2 if c == 0 else 8
            if j == 2:
                o_ = work.tile([P, 512], F32, name="o", tag="o", bufs=8)
                nc.scalar.activation(out=o_[:], in_=mm[:], func=ACT.Identity, bias=bt[:, c, 8 + un : 9 + un])
                st_prod[(i, c)] = (o_, None)
                return
            o_ = work.tile([P, 512], F32, name="o", tag="o", bufs=8)
            t_ = tsin[(c, i % 2)]
            for s_, dst in ((0, o_), (1, t_)):
                for pos in range(s_, npos):
                    nc.scalar.activation(
                        out=pos_view(dst[:], c, pos), in_=pos_view(mm[:], c, pos), func=ACT.Identity,
                        scale=cs[:, j, s_, pos : pos + 1], bias=bcs[:, s_, c, 4 * j + un, pos : pos + 1],
                    )
            st_prod[(i, c)] = (o_, t_)

        def back_t(i, a):
            tb = ps_tb.tile([P, UCOLS], F32, name="tb", tag="tb")
            toks = slice(a * P, (a + 1) * P)
            for c in range(RT):
                ya, yb = st_prod[(i, c)]
                dst = tb[:, c * P : (c + 1) * P]
                if yb is None:
                    nc.tensor.transpose(dst, ya[:, toks], ident_f[:])
                    continue
                nc.tensor.matmul(out=dst, lhsT=ya[:, toks], rhs=ident_f[:], is_transpose=True, start=True, stop=False)
                nc.tensor.matmul(out=dst, lhsT=yb[:, toks], rhs=swap_p[:], is_transpose=True, start=False, stop=True)
            return tb

        def store(i, stg):
            j, un = ORDER[i]
            for win in range(NWIN):
                nc.sync.dma_start(
                    out=outs[j][win, UH * un : UH * (un + 1)].rearrange("h (m a) e -> m h (a e)", a=4),
                    in_=stg[win : P : 4, :, :, :].rearrange("p h a e -> p h (a e)"),
                )

        def back_out(i, a, tb):
            if a == 0:
                stg_new = work.tile([P, UH, 4, HD], F32, name="stg", tag="stg", bufs=3)
                st_out[i] = stg_new
            if a in BV:
                nc.vector.tensor_copy(out=st_out[i][:, :, a, :], in_=tb[:].rearrange("p (e h) -> p h e", h=UH))
            else:
                nc.scalar.copy(out=st_out[i][:, :, a, :], in_=tb[:].rearrange("p (e h) -> p h e", h=UH))
            if a == 3:
                store(i, st_out[i])

        def v_bank(i, a):
            codes, planes = st_codes[i]
            mm = ps_mm.tile([P, 512], F32, name="mm", tag="mm")
            toks = slice(a * P, (a + 1) * P)
            for c0, cn in ((0, 256), (256, 128)):
                for g in range(PASSES):
                    nc.tensor.matmul_mx(
                        out=mm[:, c0 : c0 + cn],
                        lhsT=xcodes[:, g, toks].bitcast(FP8X4), lhsT_scale=xplanes[:, g, toks],
                        rhs=codes[:, g, c0 : c0 + cn].bitcast(FP8X4), rhs_scale=planes[:, g, c0 : c0 + cn],
                        start=(g == 0), stop=(g == PASSES - 1),
                    )
            return mm

        def v_out(i, a, mm):
            if a == 0:
                sv_new = work.tile([P, UH, 4, HD], F32, name="sv", tag="sv", bufs=3)
                st_out[i] = sv_new
            nc.vector.tensor_tensor(
                out=st_out[i][:, :, a, :], in0=mm[:, 0:UCOLS].rearrange("p (e h) -> p h e", h=UH),
                in1=bias_v[:, UH * ORDER[i][1] : UH * (ORDER[i][1] + 1), :], op=ALU.add,
            )
            if a == 3:
                store(i, st_out[i])

        cast(0, 0)
        nc.scalar.activation(out=trig[:], in_=wrap[:], func=ACT.Sin)
        cast(0, 1)
        cast(0, 2)
        trig_tables()
        bias_tables()
        for s in range(n_units + 3):
            if 1 <= s and s + 1 + AHEAD < n_units:
                load(s + 1 + AHEAD)
            if s < n_units:
                grp = work.tile([P, PASSES, 4 * UCOLS], BF16, name="grp", tag="grp", bufs=2, align_bytes=64)
                st_g[s] = grp
            for ph in range(3):
                ca = s + AHEAD
                if s > 0 and ca < n_units:
                    cast(ca, (2, 0, 1)[ph])
                jobs = []
                if s < n_units:
                    for spec in PLAN[GS[s]][ph]:
                        jobs.extend(t_bank(s, spec))
                s1, ph1 = divmod(3 * s + ph - 3 - LAG, 3)
                s2, ph2 = divmod(3 * s + ph - 6 - LAG, 3)
                if 0 <= s1 < n_units:
                    if ORDER[s1][0] == 2 and s1 not in VS:
                        for a in ((0,), (1, 2), (3,))[ph1]:
                            mm = v_bank(s1, a)
                            if jobs:
                                scaled_out(s, jobs.pop(0))
                            v_out(s1, a, mm)
                    else:
                        products(s1, ph1, mx_tile(s1, ph1))
                for job in jobs:
                    scaled_out(s, job)
                if 0 <= s2 < n_units and (ORDER[s2][0] != 2 or s2 in VS):
                    for a in ((0,), (1, 2), (3,))[ph2]:
                        back_out(s2, a, back_t(s2, a))
            if s == 0:
                for g in range(PASSES):
                    x_pass(g)
                for i in range(1, AHEAD + 1):
                    for r in (2, 0, 1):
                        cast(i, r)
            if s < n_units:
                quant(s)
            if s == 0:
                for g in range(PASSES):
                    x_quant(g)
            if s == 1:
                nc.sync.dma_start(
                    out=bias_v[:].rearrange("p h e -> p (h e)"), in_=qkv_b[2 * JROWS :].partition_broadcast(P)
                )
